import numpy as np
import ml_dtypes


def mxq(x, axis, fmt="e4m3"):
    dtype, down = {"e4m3": (ml_dtypes.float8_e4m3fn, 7), "e5m2": (ml_dtypes.float8_e5m2, 14)}[fmt]
    v = np.moveaxis(np.asarray(x, np.float32).astype(ml_dtypes.bfloat16).astype(np.float64), axis, -1)
    blocks = v.reshape(v.shape[:-1] + (-1, 32))
    amax = np.abs(blocks).max(-1, keepdims=True)
    byte = np.maximum(np.where(amax > 0, np.frexp(amax)[1] - 1 + 127, 0) - down, 1)
    scale = np.exp2(byte - 127.0)
    codes = (blocks / scale).astype(np.float32).astype(dtype).astype(np.float64)
    return np.moveaxis((codes * scale).reshape(v.shape), -1, axis)


WIDE = False


def mx_kscale(k):
    if not WIDE:
        return np.ones(k)
    levels = np.array([10, -10, 5, -5, 0])
    if k % 512:
        return np.exp2(np.random.permutation(np.resize(levels, k // 32))).repeat(32)
    a = np.empty((k // 512, 16))
    for p in range(k // 512):
        a[p, :8] = np.random.permutation(np.resize(levels, 8))
        for g in range(8):
            far = levels[np.abs(levels - a[p, g]) >= 10]
            a[p, g + 8] = far[np.random.randint(len(far))]
    return np.exp2(a.ravel()).repeat(32)


BF16 = ml_dtypes.bfloat16


def bf(x):
    return np.asarray(x, np.float32).astype(BF16)


def f64(x):
    return np.asarray(x).astype(np.float64)


B, T, C, H, W = 1, 4096, 512, 4, 512
D = C // H
HALF = D // 2
ROPE_BASE = 10000.0


def rotate_half(u):
    return np.concatenate([-u[..., HALF:], u[..., :HALF]], axis=-1)


def setup_inputs():
    s = mx_kscale(C)
    start = np.random.randint(0, T)
    inv_freq = 1.0 / (ROPE_BASE ** (np.arange(0, D, 2) / D))
    freqs = np.outer(start + np.arange(T), inv_freq)
    emb = np.concatenate([freqs, freqs], axis=-1)
    return {"x": bf(np.random.standard_normal((B, T, C)) * s),
            "freqs_cos": bf(np.cos(emb)),
            "freqs_sin": bf(np.sin(emb)),
            "w_attn": bf(np.random.standard_normal((C, 3 * C)) * 1.25 / np.sqrt(C) / s[:, None])}


def reference(x, freqs_cos, freqs_sin, w_attn):
    qkv = mxq(f64(x), 2, "e4m3") @ mxq(f64(w_attn), 0, "e4m3")
    q, k, v = np.split(qkv, 3, axis=-1)
    q = q.reshape(B, T, H, D).transpose(0, 2, 1, 3)
    k = k.reshape(B, T, H, D).transpose(0, 2, 1, 3)
    v = v.reshape(B, T, H, D).transpose(0, 2, 1, 3)
    cos = f64(freqs_cos)[None, None, :, :]
    sin = f64(freqs_sin)[None, None, :, :]
    q_rot = q * cos + rotate_half(q) * sin
    k_rot = k * cos + rotate_half(k) * sin
    return q_rot, k_rot, v

@@ -1,0 +1,187 @@
+from contextlib import ExitStack
+
+import concourse.mybir as mybir
+from concourse.masks import make_identity
+
+F32 = mybir.dt.float32
+BF16 = mybir.dt.bfloat16
+U32 = mybir.dt.uint32
+U8 = mybir.dt.uint8
+FP8X4 = mybir.dt.float8_e4m3fn_x4
+MULT = mybir.AluOpType.mult
+ADD = mybir.AluOpType.add
+SUBTRACT = mybir.AluOpType.subtract
+
+P = 128
+T = 4096
+C = 512
+PACK = 4
+HEADS = 4
+D = 128
+HALF = D // 2
+QK_HEADS = 2 * HEADS
+BANK = 512
+
+ROUNDS = T // P
+GROUP = 4
+GROUPS = ROUNDS // GROUP
+PAIR = 2
+
+FLOPS = 2 * T * C * 3 * C
+
+
+def tile_swaattention_pa_t_kernel(tc, x, freqs_cos, freqs_sin, w_attn, out_0, out_1, out_2):
+    nc = tc.nc
+
+    x_view = x.rearrange("b (p g j) c -> (b p) g (j c)", g=GROUPS, j=GROUP)
+    cos_view = freqs_cos.rearrange("(p g j) d -> p g j d", g=GROUPS, j=GROUP)
+    sin_view = freqs_sin.rearrange("(p g j) d -> p g j d", g=GROUPS, j=GROUP)
+    q_view = out_0.rearrange("b h (p g j) d -> p g (b h) j d", g=GROUPS, j=GROUP)
+    k_view = out_1.rearrange("b h (p g j) d -> p g (b h) j d", g=GROUPS, j=GROUP)
+    v_view = out_2.rearrange("b h (p g j) d -> p g (b h) j d", g=GROUPS, j=GROUP)
+
+    with ExitStack() as ctx:
+        ctx.enter_context(tc.manual_schedule())
+        const = ctx.enter_context(tc.tile_pool(name="const", bufs=1))
+        inputs = ctx.enter_context(tc.tile_pool(name="inputs", bufs=GROUPS))
+        xq = ctx.enter_context(tc.tile_pool(name="xq", bufs=2))
+        results = ctx.enter_context(tc.tile_pool(name="results", bufs=3))
+        psum_t = ctx.enter_context(tc.psum_pool(name="psum_t", bufs=2))
+        psum_mm = ctx.enter_context(tc.psum_pool(name="psum_mm", bufs=2))
+
+        w_raw = const.tile([P, PACK, 3 * C], BF16)
+        nc.sync.dma_start(out=w_raw[:], in_=w_attn.rearrange("(p t) c -> p t c", t=PACK))
+        x_in = []
+        cos_in = []
+        sin_in = []
+        for g in range(GROUPS):
+            x_g = inputs.tile([P, GROUP * C], BF16, name="x_g")
+            nc.sync.dma_start(out=x_g[:], in_=x_view[:, g, :])
+            cos_g = inputs.tile([P, GROUP, D], BF16, name="cos_g")
+            nc.sync.dma_start(out=cos_g[:], in_=cos_view[:, g])
+            sin_g = inputs.tile([P, GROUP, D], BF16, name="sin_g")
+            nc.sync.dma_start(out=sin_g[:], in_=sin_view[:, g])
+            x_in.append(x_g)
+            cos_in.append(cos_g)
+            sin_in.append(sin_g)
+
+        identity = const.tile([P, P], F32)
+        make_identity(nc, identity[:])
+
+        def transpose_group(g):
+            x_words = x_in[g][:].bitcast(F32)
+            grouped = xq.tile([P, GROUP * P * PACK], BF16, name="grouped", align_bytes=64)
+            grouped_words = grouped[:].bitcast(F32).rearrange(
+                "p (j r u) -> p j r u", j=GROUP, r=P, u=2
+            )
+            for half_group in range(GROUP // 2):
+                turned = psum_t.tile([P, 2, 2, P], F32, name="turned")
+                for i in range(2):
+                    j = 2 * half_group + i
+                    for u in range(2):
+                        first = 2 * j * P + u
+                        nc.tensor.transpose(turned[:, i, u, :], x_words[:, first : 2 * (j + 1) * P : 2], identity[:])
+                nc.scalar.copy(
+                    out=grouped_words[:, 2 * half_group : 2 * half_group + 2],
+                    in_=turned[:].rearrange("p i u r -> p i r u"),
+                )
+            return grouped
+
+        def quantise_group(grouped):
+            x_codes = xq.tile([P, GROUP * P], U32, name="x_codes", align_bytes=64)
+            x_scales = xq.tile([P, GROUP * P], U8, name="x_scales", align_bytes=64)
+            nc.vector.quantize_mx(out=x_codes[:].bitcast(FP8X4), scales=x_scales[:], in_=grouped[:])
+            return x_codes, x_scales
+
+        w_grouped = const.tile([P, 3 * BANK * PACK], BF16, align_bytes=64)
+        w_codes = const.tile([P, 3 * BANK], U32, align_bytes=64)
+        w_scales = const.tile([P, 3 * BANK], U8, align_bytes=64)
+        qk_halves = w_raw[:, :, 0 : 2 * C].rearrange("p t (n f d) -> p f n d t", f=2, d=HALF)
+
+        grouped_next = transpose_group(0)
+        for f in range(2):
+            nc.vector.tensor_copy(
+                out=w_grouped[:, f * BANK * PACK : (f + 1) * BANK * PACK].rearrange(
+                    "p (n d t) -> p n d t", n=QK_HEADS, d=HALF
+                ),
+                in_=qk_halves[:, f],
+            )
+        nc.scalar.copy(
+            out=w_grouped[:, 2 * BANK * PACK : 3 * BANK * PACK].rearrange("p (c t) -> p c t", t=PACK),
+            in_=w_raw[:, :, 2 * C : 3 * C].rearrange("p t c -> p c t"),
+        )
+        for block in (0, 1):
+            nc.vector.quantize_mx(
+                out=w_codes[:, block * BANK : (block + 1) * BANK].bitcast(FP8X4),
+                scales=w_scales[:, block * BANK : (block + 1) * BANK],
+                in_=w_grouped[:, block * BANK * PACK : (block + 1) * BANK * PACK],
+            )
+        codes_next = quantise_group(grouped_next)
+        nc.vector.quantize_mx(
+            out=w_codes[:, 2 * BANK : 3 * BANK].bitcast(FP8X4),
+            scales=w_scales[:, 2 * BANK : 3 * BANK],
+            in_=w_grouped[:, 2 * BANK * PACK : 3 * BANK * PACK],
+        )
+
+        for g in range(GROUPS):
+            last_group = g == GROUPS - 1
+            x_codes, x_scales = codes_next
+            if not last_group:
+                grouped_next = transpose_group(g + 1)
+            cos_g = cos_in[g]
+            sin_g = sin_in[g]
+            qk_main = results.tile([P, QK_HEADS, GROUP, D], F32, name="qk_main")
+            v_out = results.tile([P, HEADS, GROUP, D], F32, name="v_out")
+            for pair in range(GROUP // PAIR):
+                rounds = slice(pair * PAIR, (pair + 1) * PAIR)
+                qk_cross = results.tile([P, QK_HEADS, PAIR, D], F32, name="qk_cross")
+                for i in range(PAIR):
+                    j = pair * PAIR + i
+                    banks = []
+                    for block in range(3):
+                        acc = psum_mm.tile([P, BANK], F32, name="acc%d" % block)
+                        nc.tensor.matmul_mx(
+                            out=acc[:],
+                            lhsT=x_codes[:, j * P : (j + 1) * P].bitcast(FP8X4),
+                            lhsT_scale=x_scales[:, j * P : (j + 1) * P],
+                            rhs=w_codes[:, block * BANK : (block + 1) * BANK].bitcast(FP8X4),
+                            rhs_scale=w_scales[:, block * BANK : (block + 1) * BANK],
+                            start=True,
+                            stop=True,
+                        )
+                        banks.append(acc)
+                    low = banks[0][:].rearrange("p (n d) -> p n d", d=HALF)
+                    high = banks[1][:].rearrange("p (n d) -> p n d", d=HALF)
+
+                    def table(tab, first):
+                        return tab[:, j : j + 1, first : first + HALF].to_broadcast([P, QK_HEADS, HALF])
+
+                    nc.vector.tensor_tensor(out=qk_main[:, :, j, 0:HALF], in0=low, in1=table(cos_g, 0), op=MULT)
+                    nc.vector.tensor_tensor(out=qk_cross[:, :, i, HALF:D], in0=low, in1=table(sin_g, HALF), op=MULT)
+                    nc.vector.tensor_tensor(out=qk_main[:, :, j, HALF:D], in0=high, in1=table(cos_g, HALF), op=MULT)
+                    nc.vector.tensor_tensor(out=qk_cross[:, :, i, 0:HALF], in0=high, in1=table(sin_g, 0), op=MULT)
+                    nc.scalar.copy(out=v_out[:, :, j, :], in_=banks[2][:].rearrange("p (h d) -> p h d", d=D))
+
+                if pair == 0 and not last_group:
+                    codes_next = quantise_group(grouped_next)
+                adder = nc.vector if last_group and pair == GROUP // PAIR - 1 else nc.gpsimd
+                adder.tensor_tensor(
+                    out=qk_main[:, :, rounds, 0:HALF],
+                    in0=qk_main[:, :, rounds, 0:HALF],
+                    in1=qk_cross[:, :, :, 0:HALF],
+                    op=SUBTRACT,
+                )
+                adder.tensor_tensor(
+                    out=qk_main[:, :, rounds, HALF:D],
+                    in0=qk_main[:, :, rounds, HALF:D],
+                    in1=qk_cross[:, :, :, HALF:D],
+                    op=ADD,
+                )
+                if last_group:
+                    nc.sync.dma_start(out=v_view[:, g, :, rounds], in_=v_out[:, :, rounds])
+                    nc.sync.dma_start(out=q_view[:, g, :, rounds], in_=qk_main[:, 0:HEADS, rounds])
+                    nc.sync.dma_start(out=k_view[:, g, :, rounds], in_=qk_main[:, HEADS:QK_HEADS, rounds])
+            if not last_group:
+                nc.sync.dma_start(out=v_view[:, g], in_=v_out[:])
+                nc.sync.dma_start(out=q_view[:, g], in_=qk_main[:, 0:HEADS])
+                nc.sync.dma_start(out=k_view[:, g], in_=qk_main[:, HEADS:QK_HEADS])

@@ -10,7 +10,6 @@ U8 = mybir.dt.uint8
 FP8X4 = mybir.dt.float8_e4m3fn_x4
 MULT = mybir.AluOpType.mult
 ADD = mybir.AluOpType.add
-SUBTRACT = mybir.AluOpType.subtract
 
 P = 128
 T = 4096
@@ -19,7 +18,6 @@ PACK = 4
 HEADS = 4
 D = 128
 HALF = D // 2
-QK_HEADS = 2 * HEADS
 BANK = 512
 
 ROUNDS = T // P
@@ -34,8 +32,9 @@ def tile_swaattention_pa_t_kernel(tc, x, freqs_cos, freqs_sin, w_attn, out_0, ou
     nc = tc.nc
 
     x_view = x.rearrange("b (p g j) c -> (b p) g (j c)", g=GROUPS, j=GROUP)
-    cos_view = freqs_cos.rearrange("(p g j) d -> p g j d", g=GROUPS, j=GROUP)
-    sin_view = freqs_sin.rearrange("(p g j) d -> p g j d", g=GROUPS, j=GROUP)
+    cos_view = freqs_cos.rearrange("(p r) d -> p r d", r=ROUNDS)
+    sin_view = freqs_sin.rearrange("(p r) d -> p r d", r=ROUNDS)
+    w_view = w_attn.rearrange("(p t) c -> p t c", t=PACK)
     q_view = out_0.rearrange("b h (p g j) d -> p g (b h) j d", g=GROUPS, j=GROUP)
     k_view = out_1.rearrange("b h (p g j) d -> p g (b h) j d", g=GROUPS, j=GROUP)
     v_view = out_2.rearrange("b h (p g j) d -> p g (b h) j d", g=GROUPS, j=GROUP)
@@ -45,143 +44,224 @@ def tile_swaattention_pa_t_kernel(tc, x, freqs_cos, freqs_sin, w_attn, out_0, ou
         const = ctx.enter_context(tc.tile_pool(name="const", bufs=1))
         inputs = ctx.enter_context(tc.tile_pool(name="inputs", bufs=GROUPS))
         xq = ctx.enter_context(tc.tile_pool(name="xq", bufs=2))
+        work = ctx.enter_context(tc.tile_pool(name="work", bufs=3))
         results = ctx.enter_context(tc.tile_pool(name="results", bufs=3))
-        psum_t = ctx.enter_context(tc.psum_pool(name="psum_t", bufs=2))
-        psum_mm = ctx.enter_context(tc.psum_pool(name="psum_mm", bufs=2))
+        psum1 = ctx.enter_context(tc.psum_pool(name="psum1", bufs=1))
+        psum2 = ctx.enter_context(tc.psum_pool(name="psum2", bufs=2))
 
-        w_raw = const.tile([P, PACK, 3 * C], BF16)
-        nc.sync.dma_start(out=w_raw[:], in_=w_attn.rearrange("(p t) c -> p t c", t=PACK))
-        x_in = []
-        cos_in = []
-        sin_in = []
-        for g in range(GROUPS):
-            x_g = inputs.tile([P, GROUP * C], BF16, name="x_g")
-            nc.sync.dma_start(out=x_g[:], in_=x_view[:, g, :])
-            cos_g = inputs.tile([P, GROUP, D], BF16, name="cos_g")
-            nc.sync.dma_start(out=cos_g[:], in_=cos_view[:, g])
-            sin_g = inputs.tile([P, GROUP, D], BF16, name="sin_g")
-            nc.sync.dma_start(out=sin_g[:], in_=sin_view[:, g])
-            x_in.append(x_g)
-            cos_in.append(cos_g)
-            sin_in.append(sin_g)
+        cos_in = const.tile([P, ROUNDS, D], BF16, align_bytes=64, name="cos_in")
+        sin_in = const.tile([P, ROUNDS, D], BF16, align_bytes=64, name="sin_in")
+        x_in = [inputs.tile([P, GROUP * C], BF16, name="x_g") for g in range(GROUPS)]
+        w_raw = {}
 
-        identity = const.tile([P, P], F32)
+        def load_w(third):
+            w_raw[third] = const.tile([P, PACK, C], BF16, name="w_raw%d" % third)
+            nc.sync.dma_start(out=w_raw[third][:], in_=w_view[:, :, third * C : (third + 1) * C])
+
+        def load_x(g):
+            nc.sync.dma_start(out=x_in[g][:], in_=x_view[:, g, :])
+
+        def load_tables(rounds):
+            nc.sync.dma_start(out=cos_in[:, rounds], in_=cos_view[:, rounds])
+            nc.sync.dma_start(out=sin_in[:, rounds], in_=sin_view[:, rounds])
+
+        load_x(0)
+        load_w(1)
+        load_tables(slice(0, GROUP))
+        load_w(0)
+        load_w(2)
+        load_x(1)
+        load_tables(slice(GROUP, ROUNDS))
+        for g in range(2, GROUPS):
+            load_x(g)
+
+        identity = const.tile([P, P], F32, name="identity")
         make_identity(nc, identity[:])
+        identity_bf = const.tile([P, P], BF16, name="identity_bf")
+        nc.vector.tensor_copy(out=identity_bf[:], in_=identity[:])
+        swap = const.tile([P, P], F32, name="swap")
+        nc.vector.tensor_copy(out=swap[:, 0:HALF], in_=identity[:, HALF:D])
+        nc.vector.tensor_copy(out=swap[:, HALF:D], in_=identity[:, 0:HALF])
 
-        def transpose_group(g):
+        sin_turned = const.tile([P, ROUNDS, D], BF16, name="sin_turned")
+
+        def turn_sin(rounds):
+            nc.vector.tensor_copy(out=sin_turned[:, rounds, 0:HALF], in_=sin_in[:, rounds, HALF:D])
+            nc.vector.tensor_scalar(
+                out=sin_turned[:, rounds, HALF:D], in0=sin_in[:, rounds, 0:HALF], scalar1=-1.0, scalar2=None, op0=MULT
+            )
+
+        def transpose_x(g, half, pool, tag):
             x_words = x_in[g][:].bitcast(F32)
-            grouped = xq.tile([P, GROUP * P * PACK], BF16, name="grouped", align_bytes=64)
-            grouped_words = grouped[:].bitcast(F32).rearrange(
-                "p (j r u) -> p j r u", j=GROUP, r=P, u=2
+            turned = pool.tile([P, 2, 2, P], F32, name="turned", tag=tag)
+            for i in range(2):
+                first = (2 * half + i) * 2 * P
+                for u in range(2):
+                    nc.tensor.transpose(turned[:, i, u, :], x_words[:, first + u : first + 2 * P : 2], identity[:])
+            return turned
+
+        def group_x(grouped, half, turned):
+            words = grouped[:].bitcast(F32).rearrange("p (j r u) -> p j r u", j=GROUP, r=P, u=2)
+            nc.scalar.copy(out=words[:, 2 * half : 2 * half + 2], in_=turned[:].rearrange("p i u r -> p i r u"))
+
+        def quantise(pool, name, grouped):
+            codes = pool.tile([P, BANK], U32, name=name + "_codes", align_bytes=64)
+            scales = pool.tile([P, BANK], U8, name=name + "_scales", align_bytes=64)
+            nc.vector.quantize_mx(out=codes[:].bitcast(FP8X4), scales=scales[:], in_=grouped[:])
+            return codes, scales
+
+        def new_grouped():
+            return xq.tile([P, BANK * PACK], BF16, name="grouped", align_bytes=64)
+
+        def transpose_tables(g):
+            turned = psum1.tile([P, 2, BANK], BF16, name="turned_tables", tag="turned")
+            for t, table in enumerate((cos_in, sin_turned)):
+                for j in range(GROUP):
+                    nc.tensor.transpose(turned[:, t, j * P : (j + 1) * P], table[:, g * GROUP + j, :], identity_bf[:])
+            return turned
+
+        def copy_tables(turned):
+            tables = xq.tile([P, 2, BANK], BF16, name="tables")
+            nc.scalar.copy(out=tables[:], in_=turned[:])
+            return tables
+
+        w_grouped = {}
+
+        def group_w(third, copy):
+            w_grouped[third] = const.tile([P, BANK * PACK], BF16, align_bytes=64, name="w_grouped%d" % third)
+            copy(
+                out=w_grouped[third][:].rearrange("p (c t) -> p c t", t=PACK),
+                in_=w_raw[third][:].rearrange("p t c -> p c t"),
             )
-            for half_group in range(GROUP // 2):
-                turned = psum_t.tile([P, 2, 2, P], F32, name="turned")
-                for i in range(2):
-                    j = 2 * half_group + i
-                    for u in range(2):
-                        first = 2 * j * P + u
-                        nc.tensor.transpose(turned[:, i, u, :], x_words[:, first : 2 * (j + 1) * P : 2], identity[:])
-                nc.scalar.copy(
-                    out=grouped_words[:, 2 * half_group : 2 * half_group + 2],
-                    in_=turned[:].rearrange("p i u r -> p i r u"),
+
+        grouped = new_grouped()
+        for half, pool, tag in ((0, psum1, "turned"), (1, psum2, "k_sum")):
+            group_x(grouped, half, transpose_x(0, half, pool, tag))
+        group_w(1, nc.vector.tensor_copy)
+        turn_sin(slice(0, GROUP))
+        x_next = quantise(xq, "x", grouped)
+        wk = quantise(const, "wk", w_grouped[1])
+        tables_next = copy_tables(transpose_tables(0))
+        group_w(0, nc.vector.tensor_copy)
+        group_w(2, nc.scalar.copy)
+        wq = quantise(const, "wq", w_grouped[0])
+
+        def multiply(out, stationary, columns, moving):
+            nc.tensor.matmul_mx(
+                out=out,
+                lhsT=stationary[0][:, columns].bitcast(FP8X4),
+                lhsT_scale=stationary[1][:, columns],
+                rhs=moving[0][:].bitcast(FP8X4),
+                rhs_scale=moving[1][:],
+                start=True,
+                stop=True,
+            )
+
+        def finish_k(state):
+            products, k_out, head = state
+            k_sum = psum2.tile([P, GROUP, D], F32, name="k_sum")
+            for j in range(GROUP):
+                columns = slice(j * P, (j + 1) * P)
+                nc.tensor.matmul(
+                    out=k_sum[:, j, :], lhsT=products[:, 0, columns], rhs=identity[:], is_transpose=True, start=True, stop=False
                 )
-            return grouped
+                nc.tensor.matmul(
+                    out=k_sum[:, j, :], lhsT=products[:, 1, columns], rhs=swap[:], is_transpose=True, start=False, stop=True
+                )
+            nc.scalar.copy(out=k_out[:, head], in_=k_sum[:])
 
-        def quantise_group(grouped):
-            x_codes = xq.tile([P, GROUP * P], U32, name="x_codes", align_bytes=64)
-            x_scales = xq.tile([P, GROUP * P], U8, name="x_scales", align_bytes=64)
-            nc.vector.quantize_mx(out=x_codes[:].bitcast(FP8X4), scales=x_scales[:], in_=grouped[:])
-            return x_codes, x_scales
-
-        w_grouped = const.tile([P, 3 * BANK * PACK], BF16, align_bytes=64)
-        w_codes = const.tile([P, 3 * BANK], U32, align_bytes=64)
-        w_scales = const.tile([P, 3 * BANK], U8, align_bytes=64)
-        qk_halves = w_raw[:, :, 0 : 2 * C].rearrange("p t (n f d) -> p f n d t", f=2, d=HALF)
-
-        grouped_next = transpose_group(0)
-        for f in range(2):
-            nc.vector.tensor_copy(
-                out=w_grouped[:, f * BANK * PACK : (f + 1) * BANK * PACK].rearrange(
-                    "p (n d t) -> p n d t", n=QK_HEADS, d=HALF
-                ),
-                in_=qk_halves[:, f],
-            )
-        nc.scalar.copy(
-            out=w_grouped[:, 2 * BANK * PACK : 3 * BANK * PACK].rearrange("p (c t) -> p c t", t=PACK),
-            in_=w_raw[:, :, 2 * C : 3 * C].rearrange("p t c -> p c t"),
-        )
-        for block in (0, 1):
-            nc.vector.quantize_mx(
-                out=w_codes[:, block * BANK : (block + 1) * BANK].bitcast(FP8X4),
-                scales=w_scales[:, block * BANK : (block + 1) * BANK],
-                in_=w_grouped[:, block * BANK * PACK : (block + 1) * BANK * PACK],
-            )
-        codes_next = quantise_group(grouped_next)
-        nc.vector.quantize_mx(
-            out=w_codes[:, 2 * BANK : 3 * BANK].bitcast(FP8X4),
-            scales=w_scales[:, 2 * BANK : 3 * BANK],
-            in_=w_grouped[:, 2 * BANK * PACK : 3 * BANK * PACK],
-        )
-
+        pending_k = None
+        pending_stores = []
         for g in range(GROUPS):
             last_group = g == GROUPS - 1
-            x_codes, x_scales = codes_next
-            if not last_group:
-                grouped_next = transpose_group(g + 1)
-            cos_g = cos_in[g]
-            sin_g = sin_in[g]
-            qk_main = results.tile([P, QK_HEADS, GROUP, D], F32, name="qk_main")
+            x_codes = x_next
+            tables = tables_next
+            k_out = results.tile([P, HEADS, GROUP, D], F32, name="k_out")
+            q_out = results.tile([P, HEADS, GROUP, D], F32, name="q_out")
             v_out = results.tile([P, HEADS, GROUP, D], F32, name="v_out")
-            for pair in range(GROUP // PAIR):
-                rounds = slice(pair * PAIR, (pair + 1) * PAIR)
-                qk_cross = results.tile([P, QK_HEADS, PAIR, D], F32, name="qk_cross")
-                for i in range(PAIR):
-                    j = pair * PAIR + i
-                    banks = []
-                    for block in range(3):
-                        acc = psum_mm.tile([P, BANK], F32, name="acc%d" % block)
-                        nc.tensor.matmul_mx(
-                            out=acc[:],
-                            lhsT=x_codes[:, j * P : (j + 1) * P].bitcast(FP8X4),
-                            lhsT_scale=x_scales[:, j * P : (j + 1) * P],
-                            rhs=w_codes[:, block * BANK : (block + 1) * BANK].bitcast(FP8X4),
-                            rhs_scale=w_scales[:, block * BANK : (block + 1) * BANK],
-                            start=True,
-                            stop=True,
-                        )
-                        banks.append(acc)
-                    low = banks[0][:].rearrange("p (n d) -> p n d", d=HALF)
-                    high = banks[1][:].rearrange("p (n d) -> p n d", d=HALF)
-
-                    def table(tab, first):
-                        return tab[:, j : j + 1, first : first + HALF].to_broadcast([P, QK_HEADS, HALF])
-
-                    nc.vector.tensor_tensor(out=qk_main[:, :, j, 0:HALF], in0=low, in1=table(cos_g, 0), op=MULT)
-                    nc.vector.tensor_tensor(out=qk_cross[:, :, i, HALF:D], in0=low, in1=table(sin_g, HALF), op=MULT)
-                    nc.vector.tensor_tensor(out=qk_main[:, :, j, HALF:D], in0=high, in1=table(cos_g, HALF), op=MULT)
-                    nc.vector.tensor_tensor(out=qk_cross[:, :, i, 0:HALF], in0=high, in1=table(sin_g, 0), op=MULT)
-                    nc.scalar.copy(out=v_out[:, :, j, :], in_=banks[2][:].rearrange("p (h d) -> p h d", d=D))
-
-                if pair == 0 and not last_group:
-                    codes_next = quantise_group(grouped_next)
-                adder = nc.vector if last_group and pair == GROUP // PAIR - 1 else nc.gpsimd
-                adder.tensor_tensor(
-                    out=qk_main[:, :, rounds, 0:HALF],
-                    in0=qk_main[:, :, rounds, 0:HALF],
-                    in1=qk_cross[:, :, :, 0:HALF],
-                    op=SUBTRACT,
-                )
-                adder.tensor_tensor(
-                    out=qk_main[:, :, rounds, HALF:D],
-                    in0=qk_main[:, :, rounds, HALF:D],
-                    in1=qk_cross[:, :, :, HALF:D],
-                    op=ADD,
-                )
-                if last_group:
-                    nc.sync.dma_start(out=v_view[:, g, :, rounds], in_=v_out[:, :, rounds])
-                    nc.sync.dma_start(out=q_view[:, g, :, rounds], in_=qk_main[:, 0:HEADS, rounds])
-                    nc.sync.dma_start(out=k_view[:, g, :, rounds], in_=qk_main[:, HEADS:QK_HEADS, rounds])
             if not last_group:
-                nc.sync.dma_start(out=v_view[:, g], in_=v_out[:])
-                nc.sync.dma_start(out=q_view[:, g], in_=qk_main[:, 0:HEADS])
-                nc.sync.dma_start(out=k_view[:, g], in_=qk_main[:, HEADS:QK_HEADS])
+                grouped = new_grouped()
+            for s in range(GROUP):
+                r = g * GROUP + s
+                if s % PAIR == 0:
+                    q_cross = work.tile([P, PAIR, HEADS, D], F32, name="q_cross")
+                columns = slice(s * P, (s + 1) * P)
+                on_vector = s == GROUP - 1 or (last_group and s >= PAIR)
+                k_acc = psum2.tile([P, BANK], F32, name="k_acc")
+                multiply(k_acc[:], wk, columns, x_codes)
+                products = work.tile([P, 2, BANK], F32, name="products")
+                nc.vector.tensor_tensor(
+                    out=products[:],
+                    in0=k_acc[:].unsqueeze(1).to_broadcast([P, 2, BANK]),
+                    in1=tables[:],
+                    op=MULT,
+                )
+                if r == 0:
+                    wv = quantise(const, "wv", w_grouped[2])
+                q_acc = psum2.tile([P, HEADS, D], F32, name="q_acc")
+                multiply(q_acc[:].rearrange("p h d -> p (h d)"), x_codes, columns, wq)
+                v_acc = psum1.tile([P, HEADS, D], F32, name="v_acc")
+                multiply(v_acc[:].rearrange("p h d -> p (h d)"), x_codes, columns, wv)
+
+                nc.scalar.copy(out=v_out[:, :, s, :], in_=v_acc[:])
+                if not on_vector:
+                    q_raw = work.tile([P, HEADS, D], F32, name="q_raw")
+                    nc.scalar.copy(out=q_raw[:], in_=q_acc[:])
+
+                nc.vector.tensor_tensor(
+                    out=q_out[:, :, s, :], in0=q_acc[:], in1=cos_in[:, r : r + 1, :].to_broadcast([P, HEADS, D]), op=MULT
+                )
+
+                if on_vector:
+                    nc.vector.tensor_tensor(
+                        out=q_cross[:, s % PAIR],
+                        in0=q_acc[:],
+                        in1=sin_turned[:, r : r + 1, :].to_broadcast([P, HEADS, D]),
+                        op=MULT,
+                    )
+                else:
+                    nc.gpsimd.tensor_tensor(
+                        out=q_cross[:, s % PAIR],
+                        in0=q_raw[:],
+                        in1=sin_turned[:, r : r + 1, :].to_broadcast([P, HEADS, D]),
+                        op=MULT,
+                    )
+
+                if not last_group:
+                    if s < 2:
+                        group_x(grouped, s, transpose_x(g + 1, s, psum1, "turned"))
+                    if s == 2:
+                        tables_next = copy_tables(transpose_tables(g + 1))
+                if pending_k is not None:
+                    finish_k(pending_k)
+                pending_k = (products, k_out, s)
+                if s == 0:
+                    for store in pending_stores:
+                        nc.sync.dma_start(out=store[0], in_=store[1])
+                    pending_stores = []
+
+                if g == 0 and s == 0:
+                    turn_sin(slice(GROUP, ROUNDS))
+                if s == 2 and not last_group:
+                    x_next = quantise(xq, "x", grouped)
+
+                if s % PAIR == PAIR - 1:
+                    rounds = slice(s + 1 - PAIR, s + 1)
+                    adder = nc.vector if last_group and s == GROUP - 1 else nc.gpsimd
+                    for first, other in ((0, HALF), (HALF, 0)):
+                        adder.tensor_tensor(
+                            out=q_out[:, :, rounds, first : first + HALF],
+                            in0=q_out[:, :, rounds, first : first + HALF],
+                            in1=q_cross[:, :, :, other : other + HALF].rearrange("p i h d -> p h i d"),
+                            op=ADD,
+                        )
+                    if last_group:
+                        nc.sync.dma_start(out=v_view[:, g, :, rounds], in_=v_out[:, :, rounds])
+                        heads = slice(0, 1) if s == 1 else slice(1, 3)
+                        nc.sync.dma_start(out=k_view[:, g, heads], in_=k_out[:, heads])
+                        nc.sync.dma_start(out=q_view[:, g, :, rounds], in_=q_out[:, :, rounds])
+            if not last_group:
+                pending_stores = [(v_view[:, g], v_out[:]), (k_view[:, g], k_out[:]), (q_view[:, g], q_out[:])]
+
+        finish_k(pending_k)
+        nc.sync.dma_start(out=k_view[:, g, HEADS - 1], in_=k_out[:, HEADS - 1])

@@ -44,10 +44,12 @@ def tile_swaattention_pa_t_kernel(tc, x, freqs_cos, freqs_sin, w_attn, out_0, ou
         const = ctx.enter_context(tc.tile_pool(name="const", bufs=1))
         inputs = ctx.enter_context(tc.tile_pool(name="inputs", bufs=GROUPS))
         xq = ctx.enter_context(tc.tile_pool(name="xq", bufs=2))
-        work = ctx.enter_context(tc.tile_pool(name="work", bufs=3))
+        work = ctx.enter_context(tc.tile_pool(name="work", bufs=4))
         results = ctx.enter_context(tc.tile_pool(name="results", bufs=3))
-        psum1 = ctx.enter_context(tc.psum_pool(name="psum1", bufs=1))
-        psum2 = ctx.enter_context(tc.psum_pool(name="psum2", bufs=2))
+        psum = {
+            tag: ctx.enter_context(tc.psum_pool(name="psum_" + tag, bufs=bufs))
+            for tag, bufs in (("k_acc", 2), ("q_acc", 2), ("v_acc", 1), ("turned", 3))
+        }
 
         cos_in = const.tile([P, ROUNDS, D], BF16, align_bytes=64, name="cos_in")
         sin_in = const.tile([P, ROUNDS, D], BF16, align_bytes=64, name="sin_in")
@@ -66,13 +68,15 @@ def tile_swaattention_pa_t_kernel(tc, x, freqs_cos, freqs_sin, w_attn, out_0, ou
             nc.sync.dma_start(out=sin_in[:, rounds], in_=sin_view[:, rounds])
 
         load_x(0)
-        load_w(1)
-        load_tables(slice(0, GROUP))
         load_w(0)
         load_w(2)
+        load_tables(slice(0, GROUP))
+        load_w(1)
         load_x(1)
-        load_tables(slice(GROUP, ROUNDS))
-        for g in range(2, GROUPS):
+        load_tables(slice(GROUP, 3 * GROUP))
+        load_x(2)
+        load_tables(slice(3 * GROUP, ROUNDS))
+        for g in range(3, GROUPS):
             load_x(g)
 
         identity = const.tile([P, P], F32, name="identity")
@@ -83,6 +87,9 @@ def tile_swaattention_pa_t_kernel(tc, x, freqs_cos, freqs_sin, w_attn, out_0, ou
         nc.vector.tensor_copy(out=swap[:, 0:HALF], in_=identity[:, HALF:D])
         nc.vector.tensor_copy(out=swap[:, HALF:D], in_=identity[:, 0:HALF])
 
+        def swap_halves(view):
+            return view.rearrange("p n (f d) -> p n f d", f=2)[:, :, ::-1, :]
+
         sin_turned = const.tile([P, ROUNDS, D], BF16, name="sin_turned")
 
         def turn_sin(rounds):
@@ -91,9 +98,9 @@ def tile_swaattention_pa_t_kernel(tc, x, freqs_cos, freqs_sin, w_attn, out_0, ou
                 out=sin_turned[:, rounds, HALF:D], in0=sin_in[:, rounds, 0:HALF], scalar1=-1.0, scalar2=None, op0=MULT
             )
 
-        def transpose_x(g, half, pool, tag):
+        def transpose_x(g, half, tag):
             x_words = x_in[g][:].bitcast(F32)
-            turned = pool.tile([P, 2, 2, P], F32, name="turned", tag=tag)
+            turned = psum[tag].tile([P, 2, 2, P], F32, name="turned", tag=tag)
             for i in range(2):
                 first = (2 * half + i) * 2 * P
                 for u in range(2):
@@ -101,20 +108,17 @@ def tile_swaattention_pa_t_kernel(tc, x, freqs_cos, freqs_sin, w_attn, out_0, ou
             return turned
 
         def group_x(grouped, half, turned):
-            words = grouped[:].bitcast(F32).rearrange("p (j r u) -> p j r u", j=GROUP, r=P, u=2)
+            words = grouped.bitcast(F32).rearrange("p (j r u) -> p j r u", j=GROUP, r=P, u=2)
             nc.scalar.copy(out=words[:, 2 * half : 2 * half + 2], in_=turned[:].rearrange("p i u r -> p i r u"))
 
-        def quantise(pool, name, grouped):
-            codes = pool.tile([P, BANK], U32, name=name + "_codes", align_bytes=64)
-            scales = pool.tile([P, BANK], U8, name=name + "_scales", align_bytes=64)
+        def quantise(name, grouped, width):
+            codes = const.tile([P, width], U32, name=name + "_codes", align_bytes=64)
+            scales = const.tile([P, width], U8, name=name + "_scales", align_bytes=64)
             nc.vector.quantize_mx(out=codes[:].bitcast(FP8X4), scales=scales[:], in_=grouped[:])
             return codes, scales
 
-        def new_grouped():
-            return xq.tile([P, BANK * PACK], BF16, name="grouped", align_bytes=64)
-
         def transpose_tables(g):
-            turned = psum1.tile([P, 2, BANK], BF16, name="turned_tables", tag="turned")
+            turned = psum["turned"].tile([P, 2, BANK], BF16, name="turned_tables", tag="turned")
             for t, table in enumerate((cos_in, sin_turned)):
                 for j in range(GROUP):
                     nc.tensor.transpose(turned[:, t, j * P : (j + 1) * P], table[:, g * GROUP + j, :], identity_bf[:])
@@ -130,21 +134,29 @@ def tile_swaattention_pa_t_kernel(tc, x, freqs_cos, freqs_sin, w_attn, out_0, ou
         def group_w(third, copy):
             w_grouped[third] = const.tile([P, BANK * PACK], BF16, align_bytes=64, name="w_grouped%d" % third)
             copy(
-                out=w_grouped[third][:].rearrange("p (c t) -> p c t", t=PACK),
-                in_=w_raw[third][:].rearrange("p t c -> p c t"),
+                out=w_grouped[third][:].rearrange("p (c i t) -> p c t i", i=4, t=PACK),
+                in_=w_raw[third][:].rearrange("p t (c i) -> p c t i", i=4),
             )
 
-        grouped = new_grouped()
-        for half, pool, tag in ((0, psum1, "turned"), (1, psum2, "k_sum")):
-            group_x(grouped, half, transpose_x(0, half, pool, tag))
-        group_w(1, nc.vector.tensor_copy)
-        turn_sin(slice(0, GROUP))
-        x_next = quantise(xq, "x", grouped)
-        wk = quantise(const, "wk", w_grouped[1])
-        tables_next = copy_tables(transpose_tables(0))
-        group_w(0, nc.vector.tensor_copy)
-        group_w(2, nc.scalar.copy)
-        wq = quantise(const, "wq", w_grouped[0])
+        grouped = {}
+        x_codes = {}
+        tables = {}
+
+        def start_x(first, groups):
+            grouped[first] = xq.tile([P, groups * BANK * PACK], BF16, name="grouped", align_bytes=64, tag="grouped%d" % groups)
+
+        def turn_x(first, g, half, tag="turned"):
+            own = grouped[first][:, (g - first) * BANK * PACK : (g - first + 1) * BANK * PACK]
+            group_x(own, half, transpose_x(g, half, tag))
+
+        def quantise_x(first, groups):
+            codes, scales = quantise("x%d" % first, grouped[first], groups * BANK)
+            for i in range(groups):
+                columns = slice(i * BANK, (i + 1) * BANK)
+                x_codes[first + i] = (codes[:, columns], scales[:, columns])
+
+        def turn_tables(g):
+            tables[g] = copy_tables(transpose_tables(g))
 
         def multiply(out, stationary, columns, moving):
             nc.tensor.matmul_mx(
@@ -157,9 +169,32 @@ def tile_swaattention_pa_t_kernel(tc, x, freqs_cos, freqs_sin, w_attn, out_0, ou
                 stop=True,
             )
 
-        def finish_k(state):
-            products, k_out, head = state
-            k_sum = psum2.tile([P, GROUP, D], F32, name="k_sum")
+        q_out = {}
+        k_out = {}
+        v_out = {}
+        w = {}
+
+        def step_columns(n):
+            return n // GROUP, n % GROUP, slice(n % GROUP * P, (n % GROUP + 1) * P)
+
+        def start_k(n):
+            g, s, columns = step_columns(n)
+            if s == 0:
+                k_out[g] = results.tile([P, HEADS, GROUP, D], F32, name="k_out")
+            k_acc = psum["k_acc"].tile([P, BANK], F32, name="k_acc")
+            multiply(k_acc[:], w["k"], columns, x_codes[g])
+            products = work.tile([P, 2, BANK], F32, name="products", bufs=3)
+            nc.vector.tensor_tensor(
+                out=products[:],
+                in0=k_acc[:].unsqueeze(1).to_broadcast([P, 2, BANK]),
+                in1=tables[g][:],
+                op=MULT,
+            )
+            return products
+
+        def finish_k(n, products):
+            g, s = n // GROUP, n % GROUP
+            k_sum = psum["turned"].tile([P, GROUP, D], F32, name="k_sum", tag="turned")
             for j in range(GROUP):
                 columns = slice(j * P, (j + 1) * P)
                 nc.tensor.matmul(
@@ -168,100 +203,123 @@ def tile_swaattention_pa_t_kernel(tc, x, freqs_cos, freqs_sin, w_attn, out_0, ou
                 nc.tensor.matmul(
                     out=k_sum[:, j, :], lhsT=products[:, 1, columns], rhs=swap[:], is_transpose=True, start=False, stop=True
                 )
-            nc.scalar.copy(out=k_out[:, head], in_=k_sum[:])
+            nc.scalar.copy(out=k_out[g][:, s], in_=k_sum[:])
+            nc.sync.dma_start(out=k_view[:, g, s], in_=k_out[g][:, s])
 
-        pending_k = None
-        pending_stores = []
-        for g in range(GROUPS):
-            last_group = g == GROUPS - 1
-            x_codes = x_next
-            tables = tables_next
-            k_out = results.tile([P, HEADS, GROUP, D], F32, name="k_out")
-            q_out = results.tile([P, HEADS, GROUP, D], F32, name="q_out")
-            v_out = results.tile([P, HEADS, GROUP, D], F32, name="v_out")
-            if not last_group:
-                grouped = new_grouped()
-            for s in range(GROUP):
-                r = g * GROUP + s
-                if s % PAIR == 0:
-                    q_cross = work.tile([P, PAIR, HEADS, D], F32, name="q_cross")
-                columns = slice(s * P, (s + 1) * P)
-                on_vector = s == GROUP - 1 or (last_group and s >= PAIR)
-                k_acc = psum2.tile([P, BANK], F32, name="k_acc")
-                multiply(k_acc[:], wk, columns, x_codes)
-                products = work.tile([P, 2, BANK], F32, name="products")
-                nc.vector.tensor_tensor(
-                    out=products[:],
-                    in0=k_acc[:].unsqueeze(1).to_broadcast([P, 2, BANK]),
-                    in1=tables[:],
-                    op=MULT,
-                )
-                if r == 0:
-                    wv = quantise(const, "wv", w_grouped[2])
-                q_acc = psum2.tile([P, HEADS, D], F32, name="q_acc")
-                multiply(q_acc[:].rearrange("p h d -> p (h d)"), x_codes, columns, wq)
-                v_acc = psum1.tile([P, HEADS, D], F32, name="v_acc")
-                multiply(v_acc[:].rearrange("p h d -> p (h d)"), x_codes, columns, wv)
+        def matmul_q(n):
+            g, s, columns = step_columns(n)
+            q_acc = psum["q_acc"].tile([P, HEADS, D], F32, name="q_acc")
+            multiply(q_acc[:].rearrange("p h d -> p (h d)"), x_codes[g], columns, w["q"])
+            return q_acc
 
-                nc.scalar.copy(out=v_out[:, :, s, :], in_=v_acc[:])
-                if not on_vector:
-                    q_raw = work.tile([P, HEADS, D], F32, name="q_raw")
-                    nc.scalar.copy(out=q_raw[:], in_=q_acc[:])
+        def matmul_v(n):
+            g, s, columns = step_columns(n)
+            v_acc = psum["v_acc"].tile([P, HEADS, D], F32, name="v_acc")
+            multiply(v_acc[:].rearrange("p h d -> p (h d)"), x_codes[g], columns, w["v"])
+            if s == 0:
+                v_out[g] = results.tile([P, HEADS, GROUP, D], F32, name="v_out")
+            nc.scalar.copy(out=v_out[g][:, :, s, :], in_=v_acc[:])
 
-                nc.vector.tensor_tensor(
-                    out=q_out[:, :, s, :], in0=q_acc[:], in1=cos_in[:, r : r + 1, :].to_broadcast([P, HEADS, D]), op=MULT
-                )
+        def on_vector(n):
+            s = n % GROUP
+            return s % 2 == 1
 
-                if on_vector:
-                    nc.vector.tensor_tensor(
-                        out=q_cross[:, s % PAIR],
-                        in0=q_acc[:],
-                        in1=sin_turned[:, r : r + 1, :].to_broadcast([P, HEADS, D]),
-                        op=MULT,
-                    )
-                else:
-                    nc.gpsimd.tensor_tensor(
-                        out=q_cross[:, s % PAIR],
-                        in0=q_raw[:],
-                        in1=sin_turned[:, r : r + 1, :].to_broadcast([P, HEADS, D]),
-                        op=MULT,
-                    )
+        def multiply_q(n, q_acc):
+            g, s = n // GROUP, n % GROUP
+            if s == 0:
+                q_out[g] = results.tile([P, HEADS, GROUP, D], F32, name="q_out")
+            nc.vector.tensor_tensor(
+                out=q_out[g][:, :, s, :], in0=q_acc[:], in1=cos_in[:, n : n + 1, :].to_broadcast([P, HEADS, D]), op=MULT
+            )
+            if on_vector(n):
+                return cross_q(n, nc.vector, q_acc)
+            return None
 
-                if not last_group:
-                    if s < 2:
-                        group_x(grouped, s, transpose_x(g + 1, s, psum1, "turned"))
-                    if s == 2:
-                        tables_next = copy_tables(transpose_tables(g + 1))
-                if pending_k is not None:
-                    finish_k(pending_k)
-                pending_k = (products, k_out, s)
-                if s == 0:
-                    for store in pending_stores:
-                        nc.sync.dma_start(out=store[0], in_=store[1])
-                    pending_stores = []
+        def cross_q(n, engine, source):
+            q_cross = work.tile([P, HEADS, D], F32, name="q_cross", bufs=4)
+            engine.tensor_tensor(
+                out=q_cross[:].rearrange("p h (f d) -> p h f d", f=2),
+                in0=swap_halves(source[:]),
+                in1=swap_halves(sin_turned[:, n : n + 1, :]).to_broadcast([P, HEADS, 2, HALF]),
+                op=MULT,
+            )
+            return q_cross
 
-                if g == 0 and s == 0:
-                    turn_sin(slice(GROUP, ROUNDS))
-                if s == 2 and not last_group:
-                    x_next = quantise(xq, "x", grouped)
+        def copy_q(q_acc):
+            q_raw = work.tile([P, HEADS, D], F32, name="q_raw", bufs=4)
+            nc.scalar.copy(out=q_raw[:], in_=q_acc[:])
+            return q_raw
 
-                if s % PAIR == PAIR - 1:
-                    rounds = slice(s + 1 - PAIR, s + 1)
-                    adder = nc.vector if last_group and s == GROUP - 1 else nc.gpsimd
-                    for first, other in ((0, HALF), (HALF, 0)):
-                        adder.tensor_tensor(
-                            out=q_out[:, :, rounds, first : first + HALF],
-                            in0=q_out[:, :, rounds, first : first + HALF],
-                            in1=q_cross[:, :, :, other : other + HALF].rearrange("p i h d -> p h i d"),
-                            op=ADD,
-                        )
-                    if last_group:
-                        nc.sync.dma_start(out=v_view[:, g, :, rounds], in_=v_out[:, :, rounds])
-                        heads = slice(0, 1) if s == 1 else slice(1, 3)
-                        nc.sync.dma_start(out=k_view[:, g, heads], in_=k_out[:, heads])
-                        nc.sync.dma_start(out=q_view[:, g, :, rounds], in_=q_out[:, :, rounds])
-            if not last_group:
-                pending_stores = [(v_view[:, g], v_out[:]), (k_view[:, g], k_out[:]), (q_view[:, g], q_out[:])]
+        def add_q(n, q_cross):
+            g, s = n // GROUP, n % GROUP
+            adder = nc.vector if n >= ROUNDS - 1 else nc.gpsimd
+            adder.tensor_tensor(out=q_out[g][:, :, s], in0=q_out[g][:, :, s], in1=q_cross[:], op=ADD)
 
-        finish_k(pending_k)
-        nc.sync.dma_start(out=k_view[:, g, HEADS - 1], in_=k_out[:, HEADS - 1])
+        start_x(0, 1)
+        turn_x(0, 0, 0)
+        turn_x(0, 0, 1)
+        group_w(0, nc.vector.tensor_copy)
+        quantise_x(0, 1)
+        w["q"] = quantise("wq", w_grouped[0], BANK)
+        turn_sin(slice(0, GROUP))
+        group_w(2, nc.scalar.copy)
+
+        helpers = {}
+
+        def at(step, task, *args):
+            helpers.setdefault(step, []).append((task, args))
+
+        def prepare(third, name, copy):
+            if copy is not None:
+                group_w(third, copy)
+            w[name] = quantise("w" + name, w_grouped[third], BANK)
+
+        def plan_x(first, groups, steps, quantise_step):
+            at(steps[0], start_x, first, groups)
+            for i, step in enumerate(steps):
+                at(step, turn_x, first, first + i // 2, i % 2)
+            at(quantise_step, quantise_x, first, groups)
+
+        at(0, prepare, 2, "v", None)
+        at(1, prepare, 1, "k", nc.vector.tensor_copy)
+        at(2, turn_tables, 0)
+        at(3, turn_sin, slice(GROUP, 3 * GROUP))
+        at(5, turn_sin, slice(3 * GROUP, ROUNDS))
+        plan_x(1, 1, (1, 1), 2)
+        plan_x(2, 1, (2, 3), 5)
+        plan_x(3, 2, (4, 6, 7, 8), 10)
+        plan_x(5, 2, (12, 14, 15, 16), 18)
+        plan_x(7, 1, (20, 22), 24)
+        at(5, turn_tables, 1)
+        at(9, turn_tables, 2)
+        at(13, turn_tables, 3)
+        at(17, turn_tables, 4)
+        at(21, turn_tables, 5)
+        at(25, turn_tables, 6)
+        at(29, turn_tables, 7)
+
+        K_LAG = 4
+        V_LAG = 1
+        products = {}
+        cross = {}
+        for n in range(ROUNDS + K_LAG + 1):
+            if 0 <= n - K_LAG < ROUNDS:
+                products[n - K_LAG] = start_k(n - K_LAG)
+            if n < ROUNDS:
+                q_acc = matmul_q(n)
+            if 0 <= n - V_LAG < ROUNDS:
+                matmul_v(n - V_LAG)
+            if n < ROUNDS:
+                cross[n] = multiply_q(n, q_acc)
+            for task, args in helpers.get(n, ()):
+                task(*args)
+            if 0 <= n - K_LAG - 1:
+                finish_k(n - K_LAG - 1, products[n - K_LAG - 1])
+            if n < ROUNDS and not on_vector(n):
+                cross[n] = cross_q(n, nc.gpsimd, copy_q(q_acc))
+            if 1 <= n < ROUNDS + 1:
+                add_q(n - 1, cross[n - 1])
+            if n % GROUP == 1 and GROUP <= n and n - GROUP < ROUNDS:
+                nc.sync.dma_start(out=v_view[:, n // GROUP - 1], in_=v_out[n // GROUP - 1][:])
+            if n % GROUP == 1 and n >= GROUP:
+                nc.sync.dma_start(out=q_view[:, n // GROUP - 1], in_=q_out[n // GROUP - 1][:])

@@ -24,6 +24,8 @@ ROUNDS = T // P
 GROUP = 4
 GROUPS = ROUNDS // GROUP
 PAIR = 2
+TURNED_HEADS = 3
+UNITS = GROUPS * HEADS
 
 FLOPS = 2 * T * C * 3 * C
 
@@ -35,9 +37,9 @@ def tile_swaattention_pa_t_kernel(tc, x, freqs_cos, freqs_sin, w_attn, out_0, ou
     cos_view = freqs_cos.rearrange("(p r) d -> p r d", r=ROUNDS)
     sin_view = freqs_sin.rearrange("(p r) d -> p r d", r=ROUNDS)
     w_view = w_attn.rearrange("(p t) c -> p t c", t=PACK)
-    q_view = out_0.rearrange("b h (p g j) d -> p g (b h) j d", g=GROUPS, j=GROUP)
-    k_view = out_1.rearrange("b h (p g j) d -> p g (b h) j d", g=GROUPS, j=GROUP)
-    v_view = out_2.rearrange("b h (p g j) d -> p g (b h) j d", g=GROUPS, j=GROUP)
+    q_view = out_0.rearrange("b h (p r) d -> p (b h) r d", r=ROUNDS)
+    k_view = out_1.rearrange("b h (p r) d -> p (b h) r d", r=ROUNDS)
+    v_view = out_2.rearrange("b h (p r) d -> p (b h) r d", r=ROUNDS)
 
     with ExitStack() as ctx:
         ctx.enter_context(tc.manual_schedule())
@@ -45,7 +47,6 @@ def tile_swaattention_pa_t_kernel(tc, x, freqs_cos, freqs_sin, w_attn, out_0, ou
         inputs = ctx.enter_context(tc.tile_pool(name="inputs", bufs=GROUPS))
         xq = ctx.enter_context(tc.tile_pool(name="xq", bufs=2))
         work = ctx.enter_context(tc.tile_pool(name="work", bufs=4))
-        results = ctx.enter_context(tc.tile_pool(name="results", bufs=3))
         psum = {
             tag: ctx.enter_context(tc.psum_pool(name="psum_" + tag, bufs=bufs))
             for tag, bufs in (("k_acc", 2), ("q_acc", 2), ("v_acc", 1), ("turned", 3))
@@ -69,14 +70,16 @@ def tile_swaattention_pa_t_kernel(tc, x, freqs_cos, freqs_sin, w_attn, out_0, ou
 
         load_x(0)
         load_w(0)
-        load_w(2)
         load_tables(slice(0, GROUP))
         load_w(1)
+        load_w(2)
         load_x(1)
         load_tables(slice(GROUP, 3 * GROUP))
         load_x(2)
+        load_x(3)
+        load_x(4)
         load_tables(slice(3 * GROUP, ROUNDS))
-        for g in range(3, GROUPS):
+        for g in range(5, GROUPS):
             load_x(g)
 
         identity = const.tile([P, P], F32, name="identity")
@@ -87,9 +90,6 @@ def tile_swaattention_pa_t_kernel(tc, x, freqs_cos, freqs_sin, w_attn, out_0, ou
         nc.vector.tensor_copy(out=swap[:, 0:HALF], in_=identity[:, HALF:D])
         nc.vector.tensor_copy(out=swap[:, HALF:D], in_=identity[:, 0:HALF])
 
-        def swap_halves(view):
-            return view.rearrange("p n (f d) -> p n f d", f=2)[:, :, ::-1, :]
-
         sin_turned = const.tile([P, ROUNDS, D], BF16, name="sin_turned")
 
         def turn_sin(rounds):
@@ -98,56 +98,36 @@ def tile_swaattention_pa_t_kernel(tc, x, freqs_cos, freqs_sin, w_attn, out_0, ou
                 out=sin_turned[:, rounds, HALF:D], in0=sin_in[:, rounds, 0:HALF], scalar1=-1.0, scalar2=None, op0=MULT
             )
 
-        def transpose_x(g, half, tag):
-            x_words = x_in[g][:].bitcast(F32)
-            turned = psum[tag].tile([P, 2, 2, P], F32, name="turned", tag=tag)
-            for i in range(2):
-                first = (2 * half + i) * 2 * P
-                for u in range(2):
-                    nc.tensor.transpose(turned[:, i, u, :], x_words[:, first + u : first + 2 * P : 2], identity[:])
-            return turned
-
-        def group_x(grouped, half, turned):
-            words = grouped.bitcast(F32).rearrange("p (j r u) -> p j r u", j=GROUP, r=P, u=2)
-            nc.scalar.copy(out=words[:, 2 * half : 2 * half + 2], in_=turned[:].rearrange("p i u r -> p i r u"))
-
-        def quantise(name, grouped, width):
-            codes = const.tile([P, width], U32, name=name + "_codes", align_bytes=64)
-            scales = const.tile([P, width], U8, name=name + "_scales", align_bytes=64)
-            nc.vector.quantize_mx(out=codes[:].bitcast(FP8X4), scales=scales[:], in_=grouped[:])
-            return codes, scales
-
-        def transpose_tables(g):
-            turned = psum["turned"].tile([P, 2, BANK], BF16, name="turned_tables", tag="turned")
-            for t, table in enumerate((cos_in, sin_turned)):
-                for j in range(GROUP):
-                    nc.tensor.transpose(turned[:, t, j * P : (j + 1) * P], table[:, g * GROUP + j, :], identity_bf[:])
-            return turned
-
-        def copy_tables(turned):
-            tables = xq.tile([P, 2, BANK], BF16, name="tables")
-            nc.scalar.copy(out=tables[:], in_=turned[:])
-            return tables
-
-        w_grouped = {}
-
-        def group_w(third, copy):
-            w_grouped[third] = const.tile([P, BANK * PACK], BF16, align_bytes=64, name="w_grouped%d" % third)
-            copy(
-                out=w_grouped[third][:].rearrange("p (c i t) -> p c t i", i=4, t=PACK),
-                in_=w_raw[third][:].rearrange("p t (c i) -> p c t i", i=4),
-            )
-
         grouped = {}
         x_codes = {}
         tables = {}
+        w = {}
+        w_grouped = {}
 
-        def start_x(first, groups):
-            grouped[first] = xq.tile([P, groups * BANK * PACK], BF16, name="grouped", align_bytes=64, tag="grouped%d" % groups)
+        def quantise(name, values, width):
+            codes = const.tile([P, width], U32, name=name + "_codes", align_bytes=64)
+            scales = const.tile([P, width], U8, name=name + "_scales", align_bytes=64)
+            nc.vector.quantize_mx(out=codes[:].bitcast(FP8X4), scales=scales[:], in_=values[:])
+            return codes, scales
 
-        def turn_x(first, g, half, tag="turned"):
-            own = grouped[first][:, (g - first) * BANK * PACK : (g - first + 1) * BANK * PACK]
-            group_x(own, half, transpose_x(g, half, tag))
+        def turn_x(first, groups, i):
+            if i == 0:
+                grouped[first] = xq.tile(
+                    [P, groups * BANK * PACK],
+                    BF16,
+                    name="grouped",
+                    align_bytes=64,
+                    tag="grouped%d" % groups,
+                    bufs=3 - groups,
+                )
+            x_words = x_in[first + i // 2][:].bitcast(F32)
+            turned = psum["turned"].tile([P, 2, 2, P], F32, name="turned", tag="turned")
+            for j in range(2):
+                start = (2 * (i % 2) + j) * 2 * P
+                for u in range(2):
+                    nc.tensor.transpose(turned[:, j, u, :], x_words[:, start + u : start + 2 * P : 2], identity[:])
+            words = grouped[first][:].bitcast(F32).rearrange("p (j r u) -> p j r u", r=P, u=2)
+            nc.scalar.copy(out=words[:, 2 * i : 2 * i + 2], in_=turned[:].rearrange("p j u r -> p j r u"))
 
         def quantise_x(first, groups):
             codes, scales = quantise("x%d" % first, grouped[first], groups * BANK)
@@ -156,140 +136,157 @@ def tile_swaattention_pa_t_kernel(tc, x, freqs_cos, freqs_sin, w_attn, out_0, ou
                 x_codes[first + i] = (codes[:, columns], scales[:, columns])
 
         def turn_tables(g):
-            tables[g] = copy_tables(transpose_tables(g))
+            turned = psum["turned"].tile([P, 2, BANK], BF16, name="turned_tables", tag="turned")
+            for t, table in enumerate((cos_in, sin_turned)):
+                for j in range(GROUP):
+                    nc.tensor.transpose(turned[:, t, part(j)], table[:, g * GROUP + j, :], identity_bf[:])
+            tables[g] = xq.tile([P, 2, BANK], BF16, name="tables")
+            nc.scalar.copy(out=tables[g][:], in_=turned[:])
 
-        def multiply(out, stationary, columns, moving):
+        def group_w(third, copy):
+            w_grouped[third] = const.tile([P, BANK * PACK], BF16, align_bytes=64, name="w_grouped%d" % third)
+            copy(
+                out=w_grouped[third][:].rearrange("p (c i t) -> p c t i", i=4, t=PACK),
+                in_=w_raw[third][:].rearrange("p t (c i) -> p c t i", i=4),
+            )
+
+        def quantise_w(third, name):
+            w[name] = quantise("w" + name, w_grouped[third], BANK)
+
+        def part(i):
+            return slice(i * P, (i + 1) * P)
+
+        def rounds_of(n):
+            return slice(n // HEADS * GROUP, (n // HEADS + 1) * GROUP)
+
+        def multiply(out, stationary, columns, moving, moving_columns):
             nc.tensor.matmul_mx(
                 out=out,
                 lhsT=stationary[0][:, columns].bitcast(FP8X4),
                 lhsT_scale=stationary[1][:, columns],
-                rhs=moving[0][:].bitcast(FP8X4),
-                rhs_scale=moving[1][:],
+                rhs=moving[0][:, moving_columns].bitcast(FP8X4),
+                rhs_scale=moving[1][:, moving_columns],
                 start=True,
                 stop=True,
             )
 
-        q_out = {}
-        k_out = {}
-        v_out = {}
-        w = {}
-
-        def step_columns(n):
-            return n // GROUP, n % GROUP, slice(n % GROUP * P, (n % GROUP + 1) * P)
-
-        def start_k(n):
-            g, s, columns = step_columns(n)
-            if s == 0:
-                k_out[g] = results.tile([P, HEADS, GROUP, D], F32, name="k_out")
-            k_acc = psum["k_acc"].tile([P, BANK], F32, name="k_acc")
-            multiply(k_acc[:], w["k"], columns, x_codes[g])
-            products = work.tile([P, 2, BANK], F32, name="products", bufs=3)
-            nc.vector.tensor_tensor(
-                out=products[:],
-                in0=k_acc[:].unsqueeze(1).to_broadcast([P, 2, BANK]),
-                in1=tables[g][:],
-                op=MULT,
-            )
-            return products
-
-        def finish_k(n, products):
-            g, s = n // GROUP, n % GROUP
-            k_sum = psum["turned"].tile([P, GROUP, D], F32, name="k_sum", tag="turned")
+        def matmul_unit(n, name):
+            acc = psum[name + "_acc"].tile([P, GROUP, D], F32, name=name + "_acc")
             for j in range(GROUP):
-                columns = slice(j * P, (j + 1) * P)
-                nc.tensor.matmul(
-                    out=k_sum[:, j, :], lhsT=products[:, 0, columns], rhs=identity[:], is_transpose=True, start=True, stop=False
-                )
-                nc.tensor.matmul(
-                    out=k_sum[:, j, :], lhsT=products[:, 1, columns], rhs=swap[:], is_transpose=True, start=False, stop=True
-                )
-            nc.scalar.copy(out=k_out[g][:, s], in_=k_sum[:])
-            nc.sync.dma_start(out=k_view[:, g, s], in_=k_out[g][:, s])
+                multiply(acc[:, j, :], x_codes[n // HEADS], part(j), w[name], part(n % HEADS))
+            return acc
 
-        def matmul_q(n):
-            g, s, columns = step_columns(n)
-            q_acc = psum["q_acc"].tile([P, HEADS, D], F32, name="q_acc")
-            multiply(q_acc[:].rearrange("p h d -> p (h d)"), x_codes[g], columns, w["q"])
-            return q_acc
-
-        def matmul_v(n):
-            g, s, columns = step_columns(n)
-            v_acc = psum["v_acc"].tile([P, HEADS, D], F32, name="v_acc")
-            multiply(v_acc[:].rearrange("p h d -> p (h d)"), x_codes[g], columns, w["v"])
-            if s == 0:
-                v_out[g] = results.tile([P, HEADS, GROUP, D], F32, name="v_out")
-            nc.scalar.copy(out=v_out[g][:, :, s, :], in_=v_acc[:])
-
-        def on_vector(n):
-            s = n % GROUP
-            return s % 2 == 1
-
-        def multiply_q(n, q_acc):
-            g, s = n // GROUP, n % GROUP
-            if s == 0:
-                q_out[g] = results.tile([P, HEADS, GROUP, D], F32, name="q_out")
-            nc.vector.tensor_tensor(
-                out=q_out[g][:, :, s, :], in0=q_acc[:], in1=cos_in[:, n : n + 1, :].to_broadcast([P, HEADS, D]), op=MULT
-            )
-            if on_vector(n):
-                return cross_q(n, nc.vector, q_acc)
-            return None
-
-        def cross_q(n, engine, source):
-            q_cross = work.tile([P, HEADS, D], F32, name="q_cross", bufs=4)
+        def cross(out, source, n, engine):
             engine.tensor_tensor(
-                out=q_cross[:].rearrange("p h (f d) -> p h f d", f=2),
-                in0=swap_halves(source[:]),
-                in1=swap_halves(sin_turned[:, n : n + 1, :]).to_broadcast([P, HEADS, 2, HALF]),
+                out=out.rearrange("p j (f d) -> p j f d", f=2),
+                in0=source.rearrange("p j (f d) -> p j f d", f=2)[:, :, ::-1, :],
+                in1=sin_turned[:, rounds_of(n), :].rearrange("p j (f d) -> p j f d", f=2)[:, :, ::-1, :],
                 op=MULT,
             )
-            return q_cross
 
-        def copy_q(q_acc):
-            q_raw = work.tile([P, HEADS, D], F32, name="q_raw", bufs=4)
-            nc.scalar.copy(out=q_raw[:], in_=q_acc[:])
-            return q_raw
+        def straight(out, source, n):
+            nc.vector.tensor_tensor(out=out, in0=source, in1=cos_in[:, rounds_of(n), :], op=MULT)
 
-        def add_q(n, q_cross):
-            g, s = n // GROUP, n % GROUP
-            adder = nc.vector if n >= ROUNDS - 1 else nc.gpsimd
-            adder.tensor_tensor(out=q_out[g][:, :, s], in0=q_out[g][:, :, s], in1=q_cross[:], op=ADD)
+        def store(view, n, heads, result):
+            nc.sync.dma_start(out=view[:, n % HEADS - heads + 1 : n % HEADS + 1, rounds_of(n)], in_=result)
 
-        start_x(0, 1)
-        turn_x(0, 0, 0)
-        turn_x(0, 0, 1)
-        group_w(0, nc.vector.tensor_copy)
-        quantise_x(0, 1)
-        w["q"] = quantise("wq", w_grouped[0], BANK)
-        turn_sin(slice(0, GROUP))
-        group_w(2, nc.scalar.copy)
+        def make_v(n):
+            acc = matmul_unit(n, "v")
+            v_out = work.tile([P, 1, GROUP, D], F32, name="v_out", bufs=5)
+            nc.scalar.copy(out=v_out[:, 0], in_=acc[:])
+            return v_out
+
+        q_acc = {}
+        q_main = {}
+        q_cross = {}
+
+        def sine_on_vector(n):
+            return n % 4 != 1 or n >= UNITS - 4
+
+        def multiply_q(n):
+            if n % PAIR == 0:
+                q_main[n // PAIR] = work.tile([P, PAIR, GROUP, D], F32, name="q_main", bufs=6)
+                q_cross[n // PAIR] = work.tile([P, PAIR, GROUP, D], F32, name="q_cross", bufs=3)
+            straight(q_main[n // PAIR][:, n % PAIR], q_acc[n][:], n)
+            if sine_on_vector(n):
+                cross(q_cross[n // PAIR][:, n % PAIR], q_acc[n][:], n, nc.vector)
+
+        def cross_q_on_gpsimd(n):
+            q_raw = work.tile([P, GROUP, D], F32, name="q_raw", bufs=4)
+            nc.scalar.copy(out=q_raw[:], in_=q_acc[n][:])
+            cross(q_cross[n // PAIR][:, n % PAIR], q_raw[:], n, nc.gpsimd)
+
+        def add_q(pair, adder):
+            adder.tensor_tensor(out=q_main[pair][:], in0=q_main[pair][:], in1=q_cross[pair][:], op=ADD)
+
+        k_acc = {}
+        k_parts = {}
+
+        def matmul_k(n):
+            if n % HEADS < TURNED_HEADS:
+                k_acc[n] = psum["k_acc"].tile([P, BANK], F32, name="k_acc")
+                multiply(k_acc[n][:], w["k"], part(n % HEADS), x_codes[n // HEADS], slice(0, BANK))
+            else:
+                k_acc[n] = matmul_unit(n, "k")
+
+        def multiply_k(n):
+            acc = k_acc[n]
+            if n % HEADS < TURNED_HEADS:
+                products = work.tile([P, 2, BANK], F32, name="products", bufs=3)
+                nc.vector.tensor_tensor(
+                    out=products[:],
+                    in0=acc[:].unsqueeze(1).to_broadcast([P, 2, BANK]),
+                    in1=tables[n // HEADS][:],
+                    op=MULT,
+                )
+                k_parts[n] = products
+            else:
+                k_main = work.tile([P, 1, GROUP, D], F32, name="k_main", bufs=3)
+                k_cross = work.tile([P, GROUP, D], F32, name="k_cross", bufs=2)
+                straight(k_main[:, 0], acc[:], n)
+                cross(k_cross[:], acc[:], n, nc.vector)
+                k_parts[n] = (k_main, k_cross)
+
+        def finish_k(n, adder):
+            if n % HEADS < TURNED_HEADS:
+                products = k_parts[n]
+                k_sum = psum["turned"].tile([P, GROUP, D], F32, name="k_sum", tag="turned")
+                for j in range(GROUP):
+                    nc.tensor.matmul(
+                        out=k_sum[:, j, :], lhsT=products[:, 0, part(j)], rhs=identity[:], is_transpose=True, start=True, stop=False
+                    )
+                    nc.tensor.matmul(
+                        out=k_sum[:, j, :], lhsT=products[:, 1, part(j)], rhs=swap[:], is_transpose=True, start=False, stop=True
+                    )
+                k_main = work.tile([P, 1, GROUP, D], F32, name="k_turned", bufs=5)
+                nc.scalar.copy(out=k_main[:, 0], in_=k_sum[:])
+            else:
+                k_main, k_cross = k_parts[n]
+                adder.tensor_tensor(out=k_main[:, 0], in0=k_main[:, 0], in1=k_cross[:], op=ADD)
+            return k_main
 
         helpers = {}
 
         def at(step, task, *args):
             helpers.setdefault(step, []).append((task, args))
 
-        def prepare(third, name, copy):
-            if copy is not None:
-                group_w(third, copy)
-            w[name] = quantise("w" + name, w_grouped[third], BANK)
-
         def plan_x(first, groups, steps, quantise_step):
-            at(steps[0], start_x, first, groups)
             for i, step in enumerate(steps):
-                at(step, turn_x, first, first + i // 2, i % 2)
+                at(step, turn_x, first, groups, i)
             at(quantise_step, quantise_x, first, groups)
 
-        at(0, prepare, 2, "v", None)
-        at(1, prepare, 1, "k", nc.vector.tensor_copy)
-        at(2, turn_tables, 0)
-        at(3, turn_sin, slice(GROUP, 3 * GROUP))
+        at(0, group_w, 1, nc.scalar.copy)
+        at(0, quantise_w, 1, "k")
+        at(0, group_w, 2, nc.scalar.copy)
+        at(0, quantise_w, 2, "v")
+        at(2, turn_sin, slice(GROUP, 3 * GROUP))
         at(5, turn_sin, slice(3 * GROUP, ROUNDS))
-        plan_x(1, 1, (1, 1), 2)
-        plan_x(2, 1, (2, 3), 5)
-        plan_x(3, 2, (4, 6, 7, 8), 10)
-        plan_x(5, 2, (12, 14, 15, 16), 18)
-        plan_x(7, 1, (20, 22), 24)
+        plan_x(1, 1, (1, 2), 2)
+        plan_x(2, 1, (3, 5), 6)
+        plan_x(3, 2, (6, 7, 8, 9), 9)
+        plan_x(5, 2, (12, 13, 16, 17), 17)
+        plan_x(7, 1, (20, 23), 25)
+        at(0, turn_tables, 0)
         at(5, turn_tables, 1)
         at(9, turn_tables, 2)
         at(13, turn_tables, 3)
@@ -298,28 +295,39 @@ def tile_swaattention_pa_t_kernel(tc, x, freqs_cos, freqs_sin, w_attn, out_0, ou
         at(25, turn_tables, 6)
         at(29, turn_tables, 7)
 
-        K_LAG = 4
-        V_LAG = 1
-        products = {}
-        cross = {}
-        for n in range(ROUNDS + K_LAG + 1):
-            if 0 <= n - K_LAG < ROUNDS:
-                products[n - K_LAG] = start_k(n - K_LAG)
-            if n < ROUNDS:
-                q_acc = matmul_q(n)
-            if 0 <= n - V_LAG < ROUNDS:
-                matmul_v(n - V_LAG)
-            if n < ROUNDS:
-                cross[n] = multiply_q(n, q_acc)
+        turn_x(0, 1, 0)
+        turn_x(0, 1, 1)
+        group_w(0, nc.vector.tensor_copy)
+        quantise_x(0, 1)
+        quantise_w(0, "q")
+        turn_sin(slice(0, GROUP))
+
+        V_LAG = 2
+        K_LAG = 2
+        pending = {}
+        for n in range(UNITS + max(K_LAG, V_LAG) + 3):
+            k, q, v = n - K_LAG, n, n - V_LAG
+            if 0 <= k < UNITS:
+                matmul_k(k)
+            if 0 <= q < UNITS:
+                q_acc[q] = matmul_unit(q, "q")
+            if 0 <= v < UNITS:
+                v_out = make_v(v)
+            if 0 <= k < UNITS:
+                multiply_k(k)
+            if 0 <= q < UNITS:
+                multiply_q(q)
             for task, args in helpers.get(n, ()):
                 task(*args)
-            if 0 <= n - K_LAG - 1:
-                finish_k(n - K_LAG - 1, products[n - K_LAG - 1])
-            if n < ROUNDS and not on_vector(n):
-                cross[n] = cross_q(n, nc.gpsimd, copy_q(q_acc))
-            if 1 <= n < ROUNDS + 1:
-                add_q(n - 1, cross[n - 1])
-            if n % GROUP == 1 and GROUP <= n and n - GROUP < ROUNDS:
-                nc.sync.dma_start(out=v_view[:, n // GROUP - 1], in_=v_out[n // GROUP - 1][:])
-            if n % GROUP == 1 and n >= GROUP:
-                nc.sync.dma_start(out=q_view[:, n // GROUP - 1], in_=q_out[n // GROUP - 1][:])
+            if 0 <= k - 1 < UNITS:
+                k_main = finish_k(k - 1, nc.vector if k == UNITS else nc.gpsimd)
+                pending.setdefault(n + (2 if (k - 1) % HEADS >= TURNED_HEADS and k != UNITS else 0), []).append((k_view, k - 1, 1, k_main))
+            if 0 <= q < UNITS and not sine_on_vector(q):
+                cross_q_on_gpsimd(q)
+            if 0 <= v < UNITS:
+                store(v_view, v, 1, v_out[:])
+            if 0 <= q - 1 < UNITS and q % PAIR == 0:
+                add_q(q // PAIR - 1, nc.vector if q == UNITS else nc.gpsimd)
+                pending.setdefault(n + (0 if q == UNITS else 2), []).append((q_view, q - 1, PAIR, q_main[q // PAIR - 1]))
+            for view, unit, heads, result in pending.get(n, ()):
+                store(view, unit, heads, result[:])

@@ -170,31 +170,37 @@ def tile_swaattention_pa_t_kernel(tc, x, freqs_cos, freqs_sin, w_attn, out_0, ou
                 stop=True,
             )
 
-        def matmul_unit(n, name):
-            acc = psum[name + "_acc"].tile([P, GROUP, D], F32, name=name + "_acc")
-            for j in range(GROUP):
-                multiply(acc[:, j, :], x_codes[n // HEADS], part(j), w[name], part(n % HEADS))
+        def pair_of(n):
+            rounds = slice(n % PAIR * PAIR, n % PAIR * PAIR + PAIR)
+            heads = slice(n // PAIR % PAIR * PAIR, n // PAIR % PAIR * PAIR + PAIR)
+            return rounds, heads
+
+        def matmul_pair(n, name):
+            rounds, heads = pair_of(n)
+            acc = psum[name + "_acc"].tile([P, PAIR, PAIR, D], F32, name=name + "_acc")
+            for i in range(PAIR):
+                multiply(
+                    acc[:, i].rearrange("p h d -> p (h d)"),
+                    x_codes[n // HEADS],
+                    part(rounds.start + i),
+                    w[name],
+                    slice(heads.start * D, heads.stop * D),
+                )
             return acc
 
-        def cross(out, source, n, engine):
-            engine.tensor_tensor(
-                out=out.rearrange("p j (f d) -> p j f d", f=2),
-                in0=source.rearrange("p j (f d) -> p j f d", f=2)[:, :, ::-1, :],
-                in1=sin_turned[:, rounds_of(n), :].rearrange("p j (f d) -> p j f d", f=2)[:, :, ::-1, :],
-                op=MULT,
-            )
-
-        def straight(out, source, n):
-            nc.vector.tensor_tensor(out=out, in0=source, in1=cos_in[:, rounds_of(n), :], op=MULT)
-
         def store(view, n, heads, result):
-            nc.sync.dma_start(out=view[:, n % HEADS - heads + 1 : n % HEADS + 1, rounds_of(n)], in_=result)
+            nc.sync.dma_start(out=view[:, heads, rounds_of(n)], in_=result)
+
+        v_out = {}
 
         def make_v(n):
-            acc = matmul_unit(n, "v")
-            v_out = work.tile([P, 1, GROUP, D], F32, name="v_out", bufs=5)
-            nc.scalar.copy(out=v_out[:, 0], in_=acc[:])
-            return v_out
+            rounds, heads = pair_of(n)
+            acc = matmul_pair(n, "v")
+            if n % PAIR == 0:
+                v_out[n // PAIR] = work.tile([P, PAIR, GROUP, D], F32, name="v_out", bufs=4)
+            nc.scalar.copy(
+                out=v_out[n // PAIR][:, :, rounds].rearrange("p h j d -> p j h d"), in_=acc[:]
+            )
 
         q_acc = {}
         q_main = {}
@@ -207,17 +213,41 @@ def tile_swaattention_pa_t_kernel(tc, x, freqs_cos, freqs_sin, w_attn, out_0, ou
             if n % PAIR == 0:
                 q_main[n // PAIR] = work.tile([P, PAIR, GROUP, D], F32, name="q_main", bufs=6)
                 q_cross[n // PAIR] = work.tile([P, PAIR, GROUP, D], F32, name="q_cross", bufs=3)
-            straight(q_main[n // PAIR][:, n % PAIR], q_acc[n][:], n)
+            rounds, heads = pair_of(n)
+            first = n // HEADS * GROUP + rounds.start
+            nc.vector.tensor_tensor(
+                out=q_main[n // PAIR][:, :, rounds].rearrange("p h j d -> p j h d"),
+                in0=q_acc[n][:],
+                in1=cos_in[:, first : first + PAIR, :].unsqueeze(2).to_broadcast([P, PAIR, PAIR, D]),
+                op=MULT,
+            )
             if sine_on_vector(n):
-                cross(q_cross[n // PAIR][:, n % PAIR], q_acc[n][:], n, nc.vector)
+                cross_q(n, q_acc[n], nc.vector)
+
+        def cross_q(n, source, engine):
+            rounds, heads = pair_of(n)
+            first = n // HEADS * GROUP + rounds.start
+            engine.tensor_tensor(
+                out=q_cross[n // PAIR][:, :, rounds].rearrange("p h j d -> p j h d"),
+                in0=source[:],
+                in1=sin_turned[:, first : first + PAIR, :].unsqueeze(2).to_broadcast([P, PAIR, PAIR, D]),
+                op=MULT,
+            )
 
         def cross_q_on_gpsimd(n):
-            q_raw = work.tile([P, GROUP, D], F32, name="q_raw", bufs=4)
+            q_raw = work.tile([P, PAIR, PAIR, D], F32, name="q_raw", bufs=4)
             nc.scalar.copy(out=q_raw[:], in_=q_acc[n][:])
-            cross(q_cross[n // PAIR][:, n % PAIR], q_raw[:], n, nc.gpsimd)
+            cross_q(n, q_raw, nc.gpsimd)
+
+        def add_crossed(main, crossed, adder):
+            main = main.rearrange("p n (f d) -> p n f d", f=2)
+            crossed = crossed.rearrange("p n (f d) -> p n f d", f=2)[:, :, ::-1, :]
+            adder.tensor_tensor(out=main, in0=main, in1=crossed, op=ADD)
 
         def add_q(pair, adder):
-            adder.tensor_tensor(out=q_main[pair][:], in0=q_main[pair][:], in1=q_cross[pair][:], op=ADD)
+            add_crossed(
+                q_main[pair][:].rearrange("p h j d -> p (h j) d"), q_cross[pair][:].rearrange("p h j d -> p (h j) d"), adder
+            )
 
         k_acc = {}
         k_parts = {}
@@ -227,7 +257,9 @@ def tile_swaattention_pa_t_kernel(tc, x, freqs_cos, freqs_sin, w_attn, out_0, ou
                 k_acc[n] = psum["k_acc"].tile([P, BANK], F32, name="k_acc")
                 multiply(k_acc[n][:], w["k"], part(n % HEADS), x_codes[n // HEADS], slice(0, BANK))
             else:
-                k_acc[n] = matmul_unit(n, "k")
+                k_acc[n] = psum["k_acc"].tile([P, GROUP, D], F32, name="k_acc")
+                for j in range(GROUP):
+                    multiply(k_acc[n][:, j, :], x_codes[n // HEADS], part(j), w["k"], part(n % HEADS))
 
         def multiply_k(n):
             acc = k_acc[n]
@@ -243,8 +275,8 @@ def tile_swaattention_pa_t_kernel(tc, x, freqs_cos, freqs_sin, w_attn, out_0, ou
             else:
                 k_main = work.tile([P, 1, GROUP, D], F32, name="k_main", bufs=3)
                 k_cross = work.tile([P, GROUP, D], F32, name="k_cross", bufs=2)
-                straight(k_main[:, 0], acc[:], n)
-                cross(k_cross[:], acc[:], n, nc.vector)
+                nc.vector.tensor_tensor(out=k_main[:, 0], in0=acc[:], in1=cos_in[:, rounds_of(n), :], op=MULT)
+                nc.vector.tensor_tensor(out=k_cross[:], in0=acc[:], in1=sin_turned[:, rounds_of(n), :], op=MULT)
                 k_parts[n] = (k_main, k_cross)
 
         def finish_k(n, adder):
@@ -262,7 +294,7 @@ def tile_swaattention_pa_t_kernel(tc, x, freqs_cos, freqs_sin, w_attn, out_0, ou
                 nc.scalar.copy(out=k_main[:, 0], in_=k_sum[:])
             else:
                 k_main, k_cross = k_parts[n]
-                adder.tensor_tensor(out=k_main[:, 0], in0=k_main[:, 0], in1=k_cross[:], op=ADD)
+                add_crossed(k_main[:, 0], k_cross[:], adder)
             return k_main
 
         helpers = {}
@@ -310,9 +342,9 @@ def tile_swaattention_pa_t_kernel(tc, x, freqs_cos, freqs_sin, w_attn, out_0, ou
             if 0 <= k < UNITS:
                 matmul_k(k)
             if 0 <= q < UNITS:
-                q_acc[q] = matmul_unit(q, "q")
+                q_acc[q] = matmul_pair(q, "q")
             if 0 <= v < UNITS:
-                v_out = make_v(v)
+                make_v(v)
             if 0 <= k < UNITS:
                 multiply_k(k)
             if 0 <= q < UNITS:
@@ -321,13 +353,13 @@ def tile_swaattention_pa_t_kernel(tc, x, freqs_cos, freqs_sin, w_attn, out_0, ou
                 task(*args)
             if 0 <= k - 1 < UNITS:
                 k_main = finish_k(k - 1, nc.vector if k == UNITS else nc.gpsimd)
-                pending.setdefault(n + (2 if (k - 1) % HEADS >= TURNED_HEADS and k != UNITS else 0), []).append((k_view, k - 1, 1, k_main))
+                pending.setdefault(n + (2 if (k - 1) % HEADS >= TURNED_HEADS and k != UNITS else 0), []).append((k_view, k - 1, slice((k - 1) % HEADS, (k - 1) % HEADS + 1), k_main))
             if 0 <= q < UNITS and not sine_on_vector(q):
                 cross_q_on_gpsimd(q)
-            if 0 <= v < UNITS:
-                store(v_view, v, 1, v_out[:])
+            if 0 <= v < UNITS and v % PAIR == PAIR - 1:
+                store(v_view, v, pair_of(v)[1], v_out[v // PAIR][:])
             if 0 <= q - 1 < UNITS and q % PAIR == 0:
                 add_q(q // PAIR - 1, nc.vector if q == UNITS else nc.gpsimd)
-                pending.setdefault(n + (0 if q == UNITS else 2), []).append((q_view, q - 1, PAIR, q_main[q // PAIR - 1]))
+                pending.setdefault(n + (0 if q == UNITS else 2), []).append((q_view, q - 1, pair_of(q - 1)[1], q_main[q // PAIR - 1]))
             for view, unit, heads, result in pending.get(n, ()):
                 store(view, unit, heads, result[:])

@@ -110,6 +110,17 @@ def tile_swaattention_pa_t_kernel(tc, x, freqs_cos, freqs_sin, w_attn, out_0, ou
             nc.vector.quantize_mx(out=codes[:].bitcast(FP8X4), scales=scales[:], in_=values[:])
             return codes, scales
 
+        x_ordered = {}
+
+        def words_of_x(first, i):
+            words = x_in[first + i // 2][:].bitcast(F32).rearrange("p (j m u) -> p j u m", j=GROUP, u=2)
+            return words[:, 2 * (i % 2) : 2 * (i % 2) + 2]
+
+        def order_x(first, i):
+            ordered = xq.tile([P, 2, 2, P], F32, name="ordered", bufs=3)
+            nc.scalar.copy(out=ordered[:], in_=words_of_x(first, i))
+            x_ordered[first, i] = ordered[:]
+
         def turn_x(first, groups, i):
             if i == 0:
                 grouped[first] = xq.tile(
@@ -120,12 +131,11 @@ def tile_swaattention_pa_t_kernel(tc, x, freqs_cos, freqs_sin, w_attn, out_0, ou
                     tag="grouped%d" % groups,
                     bufs=3 - groups,
                 )
-            x_words = x_in[first + i // 2][:].bitcast(F32)
+            x_words = x_ordered[first, i] if (first, i) in x_ordered else words_of_x(first, i)
             turned = psum["turned"].tile([P, 2, 2, P], F32, name="turned", tag="turned")
             for j in range(2):
-                start = (2 * (i % 2) + j) * 2 * P
                 for u in range(2):
-                    nc.tensor.transpose(turned[:, j, u, :], x_words[:, start + u : start + 2 * P : 2], identity[:])
+                    nc.tensor.transpose(turned[:, j, u, :], x_words[:, j, u, :], identity[:])
             words = grouped[first][:].bitcast(F32).rearrange("p (j r u) -> p j r u", r=P, u=2)
             nc.scalar.copy(out=words[:, 2 * i : 2 * i + 2], in_=turned[:].rearrange("p j u r -> p j r u"))
 
@@ -304,6 +314,8 @@ def tile_swaattention_pa_t_kernel(tc, x, freqs_cos, freqs_sin, w_attn, out_0, ou
 
         def plan_x(first, groups, steps, quantise_step):
             for i, step in enumerate(steps):
+                if step >= 4:
+                    at(step - 2, order_x, first, i)
                 at(step, turn_x, first, groups, i)
             at(quantise_step, quantise_x, first, groups)
 
@@ -314,10 +326,10 @@ def tile_swaattention_pa_t_kernel(tc, x, freqs_cos, freqs_sin, w_attn, out_0, ou
         at(2, turn_sin, slice(GROUP, 3 * GROUP))
         at(5, turn_sin, slice(3 * GROUP, ROUNDS))
         plan_x(1, 1, (1, 2), 2)
-        plan_x(2, 1, (3, 5), 6)
+        plan_x(2, 1, (4, 5), 5)
         plan_x(3, 2, (6, 7, 8, 9), 9)
-        plan_x(5, 2, (12, 13, 16, 17), 17)
-        plan_x(7, 1, (20, 23), 25)
+        plan_x(5, 2, (14, 15, 16, 17), 17)
+        plan_x(7, 1, (20, 21), 21)
         at(0, turn_tables, 0)
         at(5, turn_tables, 1)
         at(9, turn_tables, 2)

@@ -52,7 +52,9 @@ def tile_swaattention_pa_t_kernel(tc, x, freqs_cos, freqs_sin, w_attn, out_0, ou
             for tag, bufs in (("k_acc", 2), ("q_acc", 2), ("v_acc", 1), ("turned", 3))
         }
 
-        cos_in = const.tile([P, ROUNDS, D], BF16, align_bytes=64, name="cos_in")
+        angles = const.tile([P, 2, ROUNDS, D], BF16, align_bytes=64, name="angles")
+        cos_in = angles[:, 0]
+        sin_turned = angles[:, 1]
         sin_in = const.tile([P, ROUNDS, D], BF16, align_bytes=64, name="sin_in")
         x_in = [inputs.tile([P, GROUP * C], BF16, name="x_g") for g in range(GROUPS)]
         w_raw = {}
@@ -90,10 +92,9 @@ def tile_swaattention_pa_t_kernel(tc, x, freqs_cos, freqs_sin, w_attn, out_0, ou
         nc.vector.tensor_copy(out=swap[:, 0:HALF], in_=identity[:, HALF:D])
         nc.vector.tensor_copy(out=swap[:, HALF:D], in_=identity[:, 0:HALF])
 
-        sin_turned = const.tile([P, ROUNDS, D], BF16, name="sin_turned")
 
         def turn_sin(rounds):
-            nc.vector.tensor_copy(out=sin_turned[:, rounds, 0:HALF], in_=sin_in[:, rounds, HALF:D])
+            nc.scalar.copy(out=sin_turned[:, rounds, 0:HALF], in_=sin_in[:, rounds, HALF:D])
             nc.vector.tensor_scalar(
                 out=sin_turned[:, rounds, HALF:D], in0=sin_in[:, rounds, 0:HALF], scalar1=-1.0, scalar2=None, op0=MULT
             )
@@ -283,11 +284,13 @@ def tile_swaattention_pa_t_kernel(tc, x, freqs_cos, freqs_sin, w_attn, out_0, ou
                 )
                 k_parts[n] = products
             else:
-                k_main = work.tile([P, 1, GROUP, D], F32, name="k_main", bufs=3)
-                k_cross = work.tile([P, GROUP, D], F32, name="k_cross", bufs=2)
-                nc.vector.tensor_tensor(out=k_main[:, 0], in0=acc[:], in1=cos_in[:, rounds_of(n), :], op=MULT)
-                nc.vector.tensor_tensor(out=k_cross[:], in0=acc[:], in1=sin_turned[:, rounds_of(n), :], op=MULT)
-                k_parts[n] = (k_main, k_cross)
+                k_parts[n] = work.tile([P, 2, GROUP, D], F32, name="k_parts", bufs=3)
+                nc.vector.tensor_tensor(
+                    out=k_parts[n][:],
+                    in0=acc[:].unsqueeze(1).to_broadcast([P, 2, GROUP, D]),
+                    in1=angles[:, :, rounds_of(n), :],
+                    op=MULT,
+                )
 
         def finish_k(n, adder):
             if n % HEADS < TURNED_HEADS:
@@ -303,9 +306,9 @@ def tile_swaattention_pa_t_kernel(tc, x, freqs_cos, freqs_sin, w_attn, out_0, ou
                 k_main = work.tile([P, 1, GROUP, D], F32, name="k_turned", bufs=5)
                 nc.scalar.copy(out=k_main[:, 0], in_=k_sum[:])
             else:
-                k_main, k_cross = k_parts[n]
-                add_crossed(k_main[:, 0], k_cross[:], adder)
-            return k_main
+                add_crossed(k_parts[n][:, 0], k_parts[n][:, 1], adder)
+                return k_parts[n][:, 0:1]
+            return k_main[:]
 
         helpers = {}
 
@@ -372,6 +375,6 @@ def tile_swaattention_pa_t_kernel(tc, x, freqs_cos, freqs_sin, w_attn, out_0, ou
                 store(v_view, v, pair_of(v)[1], v_out[v // PAIR][:])
             if 0 <= q - 1 < UNITS and q % PAIR == 0:
                 add_q(q // PAIR - 1, nc.vector if q == UNITS else nc.gpsimd)
-                pending.setdefault(n + (0 if q == UNITS else 2), []).append((q_view, q - 1, pair_of(q - 1)[1], q_main[q // PAIR - 1]))
+                pending.setdefault(n + (0 if q == UNITS else 2), []).append((q_view, q - 1, pair_of(q - 1)[1], q_main[q // PAIR - 1][:]))
             for view, unit, heads, result in pending.get(n, ()):
-                store(view, unit, heads, result[:])
+                store(view, unit, heads, result)

@@ -25,6 +25,24 @@ GROUP = 4
 GROUPS = ROUNDS // GROUP
 PAIR = 2
 TURNED_HEADS = 3
+TAILT = 1
+TAILG = 1
+LASTG = 2
+TAILS = 1
+VX = (22, 24, 26)
+VPOOL = "turned"
+VPOS = 0
+TAILCUT = 1
+SPQ = 2
+K_LAG = 2
+V_LAG = 3
+TAILSEQ = ((28, 30, 28), (29, None, 29), (30, None, 30), (31, 31, 31))
+SINA = 1
+QK = 1
+QV = 1
+GK = 0
+GV = 0
+XPLAN = ((1, 1, (1, 2), 2), (2, 1, (4, 5), 5), (3, 2, (6, 7, 8, 9), 9), (5, 2, (14, 15, 16, 17), 17), (7, 1, (20, 21), 21))
 UNITS = GROUPS * HEADS
 
 FLOPS = 2 * T * C * 3 * C
@@ -59,19 +77,26 @@ def tile_swaattention_pa_t_kernel(tc, x, freqs_cos, freqs_sin, w_attn, out_0, ou
         x_in = [inputs.tile([P, GROUP * C], BF16, name="x_g") for g in range(GROUPS)]
         w_raw = {}
 
-        def load_w(third):
-            w_raw[third] = const.tile([P, PACK, C], BF16, name="w_raw%d" % third)
-            nc.sync.dma_start(out=w_raw[third][:], in_=w_view[:, :, third * C : (third + 1) * C])
+        def load_w(third, columns=slice(0, C)):
+            if third not in w_raw:
+                w_raw[third] = const.tile([P, PACK, C], BF16, name="w_raw%d" % third)
+            nc.sync.dma_start(
+                out=w_raw[third][:, :, columns], in_=w_view[:, :, third * C + columns.start : third * C + columns.stop]
+            )
 
-        def load_x(g):
-            nc.sync.dma_start(out=x_in[g][:], in_=x_view[:, g, :])
+        def load_x(g, columns=slice(0, GROUP * C)):
+            nc.sync.dma_start(out=x_in[g][:, columns], in_=x_view[:, g, columns])
 
         def load_tables(rounds):
             nc.sync.dma_start(out=cos_in[:, rounds], in_=cos_view[:, rounds])
             nc.sync.dma_start(out=sin_in[:, rounds], in_=sin_view[:, rounds])
 
-        load_x(0)
-        load_w(0)
+        HALF_W = C // 2
+        HALF_X = GROUP * C // 2
+        load_w(0, slice(0, HALF_W))
+        load_x(0, slice(0, HALF_X))
+        load_w(0, slice(HALF_W, C))
+        load_x(0, slice(HALF_X, 2 * HALF_X))
         load_tables(slice(0, GROUP))
         load_w(1)
         load_w(2)
@@ -95,9 +120,12 @@ def tile_swaattention_pa_t_kernel(tc, x, freqs_cos, freqs_sin, w_attn, out_0, ou
 
         def turn_sin(rounds):
             nc.scalar.copy(out=sin_turned[:, rounds, 0:HALF], in_=sin_in[:, rounds, HALF:D])
-            nc.vector.tensor_scalar(
-                out=sin_turned[:, rounds, HALF:D], in0=sin_in[:, rounds, 0:HALF], scalar1=-1.0, scalar2=None, op0=MULT
-            )
+            if SINA:
+                nc.scalar.mul(sin_turned[:, rounds, HALF:D], sin_in[:, rounds, 0:HALF], -1.0)
+            else:
+                nc.vector.tensor_scalar(
+                    out=sin_turned[:, rounds, HALF:D], in0=sin_in[:, rounds, 0:HALF], scalar1=-1.0, scalar2=None, op0=MULT
+                )
 
         grouped = {}
         x_codes = {}
@@ -105,10 +133,19 @@ def tile_swaattention_pa_t_kernel(tc, x, freqs_cos, freqs_sin, w_attn, out_0, ou
         w = {}
         w_grouped = {}
 
-        def quantise(name, values, width):
-            codes = const.tile([P, width], U32, name=name + "_codes", align_bytes=64)
-            scales = const.tile([P, width], U8, name=name + "_scales", align_bytes=64)
-            nc.vector.quantize_mx(out=codes[:].bitcast(FP8X4), scales=scales[:], in_=values[:])
+        quantised = {}
+
+        def quantise(name, values, width, columns=None):
+            if name not in quantised:
+                quantised[name] = (
+                    const.tile([P, width], U32, name=name + "_codes", align_bytes=64),
+                    const.tile([P, width], U8, name=name + "_scales", align_bytes=64),
+                )
+            codes, scales = quantised[name]
+            c = columns or slice(0, width)
+            nc.vector.quantize_mx(
+                out=codes[:, c].bitcast(FP8X4), scales=scales[:, c], in_=values[:, c.start * PACK : c.stop * PACK]
+            )
             return codes, scales
 
         x_ordered = {}
@@ -140,8 +177,8 @@ def tile_swaattention_pa_t_kernel(tc, x, freqs_cos, freqs_sin, w_attn, out_0, ou
             words = grouped[first][:].bitcast(F32).rearrange("p (j r u) -> p j r u", r=P, u=2)
             nc.scalar.copy(out=words[:, 2 * i : 2 * i + 2], in_=turned[:].rearrange("p j u r -> p j r u"))
 
-        def quantise_x(first, groups):
-            codes, scales = quantise("x%d" % first, grouped[first], groups * BANK)
+        def quantise_x(first, groups, columns=None):
+            codes, scales = quantise("x%d" % first, grouped[first], groups * BANK, columns)
             for i in range(groups):
                 columns = slice(i * BANK, (i + 1) * BANK)
                 x_codes[first + i] = (codes[:, columns], scales[:, columns])
@@ -154,15 +191,16 @@ def tile_swaattention_pa_t_kernel(tc, x, freqs_cos, freqs_sin, w_attn, out_0, ou
             tables[g] = xq.tile([P, 2, BANK], BF16, name="tables")
             nc.scalar.copy(out=tables[g][:], in_=turned[:])
 
-        def group_w(third, copy):
-            w_grouped[third] = const.tile([P, BANK * PACK], BF16, align_bytes=64, name="w_grouped%d" % third)
+        def group_w(third, copy, columns=slice(0, C)):
+            if third not in w_grouped:
+                w_grouped[third] = const.tile([P, BANK * PACK], BF16, align_bytes=64, name="w_grouped%d" % third)
             copy(
-                out=w_grouped[third][:].rearrange("p (c i t) -> p c t i", i=4, t=PACK),
-                in_=w_raw[third][:].rearrange("p t (c i) -> p c t i", i=4),
+                out=w_grouped[third][:, columns.start * PACK : columns.stop * PACK].rearrange("p (c i t) -> p c t i", i=4, t=PACK),
+                in_=w_raw[third][:, :, columns].rearrange("p t (c i) -> p c t i", i=4),
             )
 
-        def quantise_w(third, name):
-            w[name] = quantise("w" + name, w_grouped[third], BANK)
+        def quantise_w(third, name, columns=None):
+            w[name] = quantise("w" + name, w_grouped[third], BANK, columns)
 
         def part(i):
             return slice(i * P, (i + 1) * P)
@@ -186,9 +224,12 @@ def tile_swaattention_pa_t_kernel(tc, x, freqs_cos, freqs_sin, w_attn, out_0, ou
             heads = slice(n // PAIR % PAIR * PAIR, n // PAIR % PAIR * PAIR + PAIR)
             return rounds, heads
 
-        def matmul_pair(n, name):
+        def matmul_pair(n, name, pool=None):
             rounds, heads = pair_of(n)
-            acc = psum[name + "_acc"].tile([P, PAIR, PAIR, D], F32, name=name + "_acc")
+            if pool:
+                acc = psum[pool].tile([P, PAIR, PAIR, D], F32, name=name + "_extra", tag=pool)
+            else:
+                acc = psum[name + "_acc"].tile([P, PAIR, PAIR, D], F32, name=name + "_acc")
             for i in range(PAIR):
                 multiply(
                     acc[:, i].rearrange("p h d -> p (h d)"),
@@ -199,14 +240,15 @@ def tile_swaattention_pa_t_kernel(tc, x, freqs_cos, freqs_sin, w_attn, out_0, ou
                 )
             return acc
 
-        def store(view, n, heads, result):
-            nc.sync.dma_start(out=view[:, heads, rounds_of(n)], in_=result)
+        def store(view, n, heads, result, rounds=slice(0, GROUP)):
+            first = n // HEADS * GROUP
+            nc.sync.dma_start(out=view[:, heads, first + rounds.start : first + rounds.stop], in_=result)
 
         v_out = {}
 
-        def make_v(n):
+        def make_v(n, pool=None):
             rounds, heads = pair_of(n)
-            acc = matmul_pair(n, "v")
+            acc = matmul_pair(n, "v", pool)
             if n % PAIR == 0:
                 v_out[n // PAIR] = work.tile([P, PAIR, GROUP, D], F32, name="v_out", bufs=4)
             nc.scalar.copy(
@@ -218,7 +260,7 @@ def tile_swaattention_pa_t_kernel(tc, x, freqs_cos, freqs_sin, w_attn, out_0, ou
         q_cross = {}
 
         def sine_on_vector(n):
-            return n % 4 != 1 or n >= UNITS - 4
+            return n % 4 != 1 or n >= UNITS - LASTG
 
         def multiply_q(n):
             if n % PAIR == 0:
@@ -263,8 +305,11 @@ def tile_swaattention_pa_t_kernel(tc, x, freqs_cos, freqs_sin, w_attn, out_0, ou
         k_acc = {}
         k_parts = {}
 
+        def is_turned(n):
+            return n % HEADS < TURNED_HEADS or (TAILT and n >= UNITS - HEADS)
+
         def matmul_k(n):
-            if n % HEADS < TURNED_HEADS:
+            if is_turned(n):
                 k_acc[n] = psum["k_acc"].tile([P, BANK], F32, name="k_acc")
                 multiply(k_acc[n][:], w["k"], part(n % HEADS), x_codes[n // HEADS], slice(0, BANK))
             else:
@@ -274,7 +319,7 @@ def tile_swaattention_pa_t_kernel(tc, x, freqs_cos, freqs_sin, w_attn, out_0, ou
 
         def multiply_k(n):
             acc = k_acc[n]
-            if n % HEADS < TURNED_HEADS:
+            if is_turned(n):
                 products = work.tile([P, 2, BANK], F32, name="products", bufs=3)
                 nc.vector.tensor_tensor(
                     out=products[:],
@@ -293,7 +338,7 @@ def tile_swaattention_pa_t_kernel(tc, x, freqs_cos, freqs_sin, w_attn, out_0, ou
                 )
 
         def finish_k(n, adder):
-            if n % HEADS < TURNED_HEADS:
+            if is_turned(n):
                 products = k_parts[n]
                 k_sum = psum["turned"].tile([P, GROUP, D], F32, name="k_sum", tag="turned")
                 for j in range(GROUP):
@@ -322,17 +367,14 @@ def tile_swaattention_pa_t_kernel(tc, x, freqs_cos, freqs_sin, w_attn, out_0, ou
                 at(step, turn_x, first, groups, i)
             at(quantise_step, quantise_x, first, groups)
 
-        at(0, group_w, 1, nc.scalar.copy)
-        at(0, quantise_w, 1, "k")
-        at(0, group_w, 2, nc.scalar.copy)
-        at(0, quantise_w, 2, "v")
+        at(GK, group_w, 1, nc.scalar.copy)
+        at(QK, quantise_w, 1, "k")
+        at(GV, group_w, 2, nc.scalar.copy)
+        at(QV, quantise_w, 2, "v")
         at(2, turn_sin, slice(GROUP, 3 * GROUP))
         at(5, turn_sin, slice(3 * GROUP, ROUNDS))
-        plan_x(1, 1, (1, 2), 2)
-        plan_x(2, 1, (4, 5), 5)
-        plan_x(3, 2, (6, 7, 8, 9), 9)
-        plan_x(5, 2, (14, 15, 16, 17), 17)
-        plan_x(7, 1, (20, 21), 21)
+        for plan in XPLAN:
+            plan_x(*plan)
         at(0, turn_tables, 0)
         at(5, turn_tables, 1)
         at(9, turn_tables, 2)
@@ -342,39 +384,69 @@ def tile_swaattention_pa_t_kernel(tc, x, freqs_cos, freqs_sin, w_attn, out_0, ou
         at(25, turn_tables, 6)
         at(29, turn_tables, 7)
 
-        turn_x(0, 1, 0)
-        turn_x(0, 1, 1)
-        group_w(0, nc.vector.tensor_copy)
-        quantise_x(0, 1)
-        quantise_w(0, "q")
+        for i in range(2):
+            half = slice(i * BANK // 2, (i + 1) * BANK // 2)
+            turn_x(0, 1, i)
+            group_w(0, nc.vector.tensor_copy, half)
+            quantise_w(0, "q", half)
+            quantise_x(0, 1, half)
         turn_sin(slice(0, GROUP))
 
-        V_LAG = 2
-        K_LAG = 2
         pending = {}
-        for n in range(UNITS + max(K_LAG, V_LAG) + 3):
-            k, q, v = n - K_LAG, n, n - V_LAG
-            if 0 <= k < UNITS:
+        steps = []
+        for n in range(UNITS + K_LAG):
+            steps.append((n - K_LAG if n >= K_LAG else None, n if n < UNITS else None, n - V_LAG if V_LAG <= n < UNITS + V_LAG else None))
+        if TAILSEQ:
+            del_ = steps.index((UNITS - 1 - K_LAG, UNITS - 1, UNITS - 1 - V_LAG))
+            steps = steps[: del_ - TAILCUT] + list(TAILSEQ)
+        steps += [(None, None, None)] * 4
+        last_ks = []
+        q_done = None
+        next_v = 0
+        for n, (k_, q, v_) in enumerate(steps):
+            ks = [k_] if k_ is not None else []
+            vs = []
+            if n >= V_LAG and next_v < UNITS:
+                vs = list(range(next_v, min(UNITS, next_v + 1 + (n in VX))))
+                next_v += len(vs)
+            for k in ks:
                 matmul_k(k)
-            if 0 <= q < UNITS:
+            if q is not None:
                 q_acc[q] = matmul_pair(q, "q")
-            if 0 <= v < UNITS:
+            for v in vs[:1]:
                 make_v(v)
-            if 0 <= k < UNITS:
+            for k in ks:
                 multiply_k(k)
-            if 0 <= q < UNITS:
+            if q is not None:
                 multiply_q(q)
             for task, args in helpers.get(n, ()):
                 task(*args)
-            if 0 <= k - 1 < UNITS:
-                k_main = finish_k(k - 1, nc.vector if k == UNITS else nc.gpsimd)
-                pending.setdefault(n + (2 if (k - 1) % HEADS >= TURNED_HEADS and k != UNITS else 0), []).append((k_view, k - 1, slice((k - 1) % HEADS, (k - 1) % HEADS + 1), k_main))
-            if 0 <= q < UNITS and not sine_on_vector(q):
+            for k in last_ks:
+                k_main = finish_k(k, nc.gpsimd)
+                pending.setdefault(n + (0 if is_turned(k) else 2), []).append((k_view, k, slice(k % HEADS, k % HEADS + 1), k_main, slice(0, GROUP)))
+            last_ks = ks
+            for v in vs[1:]:
+                make_v(v, VPOOL)
+            if q is not None and not sine_on_vector(q):
                 cross_q_on_gpsimd(q)
-            if 0 <= v < UNITS and v % PAIR == PAIR - 1:
-                store(v_view, v, pair_of(v)[1], v_out[v // PAIR][:])
-            if 0 <= q - 1 < UNITS and q % PAIR == 0:
-                add_q(q // PAIR - 1, nc.vector if q == UNITS else nc.gpsimd)
-                pending.setdefault(n + (0 if q == UNITS else 2), []).append((q_view, q - 1, pair_of(q - 1)[1], q_main[q // PAIR - 1][:]))
-            for view, unit, heads, result in pending.get(n, ()):
-                store(view, unit, heads, result)
+            for v in vs:
+                if v % PAIR == PAIR - 1:
+                    store(v_view, v, pair_of(v)[1], v_out[v // PAIR][:])
+            unit = q_done
+            if unit is not None and TAILG and unit >= UNITS - 2:
+                pair = unit // PAIR
+                rounds, heads = pair_of(unit)
+                last = unit == UNITS - 1
+                for h in range(PAIR):
+                    add_crossed(q_main[pair][:, h, rounds], q_cross[pair][:, h, rounds], nc.vector if last else nc.gpsimd)
+                if TAILS:
+                    pending.setdefault(n + (0 if last else 1), []).append((q_view, unit, heads, q_main[pair][:, :, rounds], rounds))
+                elif last:
+                    pending.setdefault(n, []).append((q_view, unit, heads, q_main[pair][:], slice(0, GROUP)))
+            elif unit is not None and unit % PAIR == PAIR - 1:
+                pair = unit // PAIR
+                add_q(pair, nc.vector if unit == UNITS - 1 else nc.gpsimd)
+                pending.setdefault(n + (0 if unit == UNITS - 1 else SPQ), []).append((q_view, unit, pair_of(unit)[1], q_main[pair][:], slice(0, GROUP)))
+            q_done = q
+            for view, unit, heads, result, rounds in pending.get(n, ()):
+                store(view, unit, heads, result, rounds)

@@ -27,7 +27,7 @@ PAIR = 2
 TURNED_HEADS = 3
 TAILT = 1
 TAILG = 1
-LASTG = 2
+LASTG = 4
 TAILS = 1
 VX = (22, 24, 26)
 VPOOL = "turned"
@@ -37,12 +37,18 @@ SPQ = 2
 K_LAG = 2
 V_LAG = 3
 TAILSEQ = ((28, 30, 28), (29, None, 29), (30, None, 30), (31, 31, 31))
-SINA = 1
+SINA = 2
+SINS = ((1, (4, 12)), (5, (12, 20)), (9, (20, 32)))
 QK = 1
 QV = 1
 GK = 0
+FS = 5
+FE = 99
+FP = 1
+PB = 5
+VP2 = 1
 GV = 0
-XPLAN = ((1, 1, (1, 2), 2), (2, 1, (4, 5), 5), (3, 2, (6, 7, 8, 9), 9), (5, 2, (14, 15, 16, 17), 17), (7, 1, (20, 21), 21))
+XPLAN = [(1,1,(1,2),2),(2,1,(4,5),5),(3,1,(6,6),9),(4,1,(10,10),13),(5,1,(14,14),17),(6,1,(18,18),21),(7,1,(22,22),25)]
 UNITS = GROUPS * HEADS
 
 FLOPS = 2 * T * C * 3 * C
@@ -119,13 +125,17 @@ def tile_swaattention_pa_t_kernel(tc, x, freqs_cos, freqs_sin, w_attn, out_0, ou
 
 
         def turn_sin(rounds):
-            nc.scalar.copy(out=sin_turned[:, rounds, 0:HALF], in_=sin_in[:, rounds, HALF:D])
-            if SINA:
-                nc.scalar.mul(sin_turned[:, rounds, HALF:D], sin_in[:, rounds, 0:HALF], -1.0)
+            first, second = sin_turned[:, rounds, 0:HALF], sin_turned[:, rounds, HALF:D]
+            if SINA == 3:
+                nc.gpsimd.tensor_scalar(out=first, in0=sin_in[:, rounds, HALF:D], scalar1=1.0, scalar2=0.0, op0=MULT, op1=ADD)
             else:
-                nc.vector.tensor_scalar(
-                    out=sin_turned[:, rounds, HALF:D], in0=sin_in[:, rounds, 0:HALF], scalar1=-1.0, scalar2=None, op0=MULT
-                )
+                nc.scalar.copy(out=first, in_=sin_in[:, rounds, HALF:D])
+            if SINA >= 2:
+                nc.gpsimd.tensor_scalar(out=second, in0=sin_in[:, rounds, 0:HALF], scalar1=-1.0, scalar2=0.0, op0=MULT, op1=ADD)
+            elif SINA == 1:
+                nc.scalar.mul(second, sin_in[:, rounds, 0:HALF], -1.0)
+            else:
+                nc.vector.tensor_scalar(out=second, in0=sin_in[:, rounds, 0:HALF], scalar1=-1.0, scalar2=None, op0=MULT)
 
         grouped = {}
         x_codes = {}
@@ -320,7 +330,7 @@ def tile_swaattention_pa_t_kernel(tc, x, freqs_cos, freqs_sin, w_attn, out_0, ou
         def multiply_k(n):
             acc = k_acc[n]
             if is_turned(n):
-                products = work.tile([P, 2, BANK], F32, name="products", bufs=3)
+                products = work.tile([P, 2, BANK], F32, name="products", bufs=PB)
                 nc.vector.tensor_tensor(
                     out=products[:],
                     in0=acc[:].unsqueeze(1).to_broadcast([P, 2, BANK]),
@@ -356,6 +366,7 @@ def tile_swaattention_pa_t_kernel(tc, x, freqs_cos, freqs_sin, w_attn, out_0, ou
             return k_main[:]
 
         helpers = {}
+        after = {}
 
         def at(step, task, *args):
             helpers.setdefault(step, []).append((task, args))
@@ -365,14 +376,14 @@ def tile_swaattention_pa_t_kernel(tc, x, freqs_cos, freqs_sin, w_attn, out_0, ou
                 if step >= 4:
                     at(step - 2, order_x, first, i)
                 at(step, turn_x, first, groups, i)
-            at(quantise_step, quantise_x, first, groups)
+            after.setdefault(quantise_step, []).append((quantise_x, (first, groups)))
 
         at(GK, group_w, 1, nc.scalar.copy)
         at(QK, quantise_w, 1, "k")
         at(GV, group_w, 2, nc.scalar.copy)
         at(QV, quantise_w, 2, "v")
-        at(2, turn_sin, slice(GROUP, 3 * GROUP))
-        at(5, turn_sin, slice(3 * GROUP, ROUNDS))
+        for step, rounds in SINS:
+            at(step, turn_sin, slice(*rounds))
         for plan in XPLAN:
             plan_x(*plan)
         at(0, turn_tables, 0)
@@ -401,6 +412,8 @@ def tile_swaattention_pa_t_kernel(tc, x, freqs_cos, freqs_sin, w_attn, out_0, ou
             steps = steps[: del_ - TAILCUT] + list(TAILSEQ)
         steps += [(None, None, None)] * 4
         last_ks = []
+        waiting_ks = []
+        waiting_turns = []
         q_done = None
         next_v = 0
         for n, (k_, q, v_) in enumerate(steps):
@@ -414,16 +427,31 @@ def tile_swaattention_pa_t_kernel(tc, x, freqs_cos, freqs_sin, w_attn, out_0, ou
             if q is not None:
                 q_acc[q] = matmul_pair(q, "q")
             for v in vs[:1]:
-                make_v(v)
+                make_v(v, VPOOL if VP2 and n >= FS and n % 2 == VP2 - 1 else None)
             for k in ks:
                 multiply_k(k)
             if q is not None:
                 multiply_q(q)
             for task, args in helpers.get(n, ()):
+                if task in (turn_x, turn_tables) and n >= FS:
+                    waiting_turns.append((task, args))
+                else:
+                    task(*args)
+            flush = n < FS or n % 2 == FP or n >= FE
+            if flush:
+                for task, args in waiting_turns:
+                    task(*args)
+                waiting_turns = []
+            for task, args in after.get(n, ()):
                 task(*args)
-            for k in last_ks:
+            rest = []
+            for k in waiting_ks + last_ks:
+                if is_turned(k) and not flush:
+                    rest.append(k)
+                    continue
                 k_main = finish_k(k, nc.gpsimd)
                 pending.setdefault(n + (0 if is_turned(k) else 2), []).append((k_view, k, slice(k % HEADS, k % HEADS + 1), k_main, slice(0, GROUP)))
+            waiting_ks = rest
             last_ks = ks
             for v in vs[1:]:
                 make_v(v, VPOOL)

from contextlib import ExitStack

import concourse.mybir as mybir
from concourse.masks import make_identity

F32 = mybir.dt.float32
BF16 = mybir.dt.bfloat16
U32 = mybir.dt.uint32
U8 = mybir.dt.uint8
FP8X4 = mybir.dt.float8_e4m3fn_x4
MULT = mybir.AluOpType.mult
ADD = mybir.AluOpType.add

P = 128
T = 4096
C = 512
PACK = 4
HEADS = 4
D = 128
HALF = D // 2
BANK = 512

ROUNDS = T // P
GROUP = 4
GROUPS = ROUNDS // GROUP
PAIR = 2
TURNED_HEADS = 3
TAILT = 1
TAILG = 1
LASTG = 4
TAILS = 1
VX = (22, 24, 26)
VPOOL = "turned"
VPOS = 0
TAILCUT = 1
SPQ = 2
K_LAG = 2
V_LAG = 3
TAILSEQ = ((28, 30, 28), (29, None, 29), (30, None, 30), (31, 31, 31))
SINA = 2
SINS = ((1, (4, 12)), (5, (12, 20)), (9, (20, 32)))
QK = 1
QV = 1
GK = 0
FS = 5
FE = 99
FP = 1
PB = 5
VP2 = 1
GV = 0
XPLAN = [(1,1,(1,2),2),(2,1,(4,5),5),(3,1,(6,6),9),(4,1,(10,10),13),(5,1,(14,14),17),(6,1,(18,18),21),(7,1,(22,22),25)]
UNITS = GROUPS * HEADS

FLOPS = 2 * T * C * 3 * C


def tile_swaattention_pa_t_kernel(tc, x, freqs_cos, freqs_sin, w_attn, out_0, out_1, out_2):
    nc = tc.nc

    x_view = x.rearrange("b (p g j) c -> (b p) g (j c)", g=GROUPS, j=GROUP)
    cos_view = freqs_cos.rearrange("(p r) d -> p r d", r=ROUNDS)
    sin_view = freqs_sin.rearrange("(p r) d -> p r d", r=ROUNDS)
    w_view = w_attn.rearrange("(p t) c -> p t c", t=PACK)
    q_view = out_0.rearrange("b h (p r) d -> p (b h) r d", r=ROUNDS)
    k_view = out_1.rearrange("b h (p r) d -> p (b h) r d", r=ROUNDS)
    v_view = out_2.rearrange("b h (p r) d -> p (b h) r d", r=ROUNDS)

    with ExitStack() as ctx:
        ctx.enter_context(tc.manual_schedule())
        const = ctx.enter_context(tc.tile_pool(name="const", bufs=1))
        inputs = ctx.enter_context(tc.tile_pool(name="inputs", bufs=GROUPS))
        xq = ctx.enter_context(tc.tile_pool(name="xq", bufs=2))
        work = ctx.enter_context(tc.tile_pool(name="work", bufs=4))
        psum = {
            tag: ctx.enter_context(tc.psum_pool(name="psum_" + tag, bufs=bufs))
            for tag, bufs in (("k_acc", 2), ("q_acc", 2), ("v_acc", 1), ("turned", 3))
        }

        angles = const.tile([P, 2, ROUNDS, D], BF16, align_bytes=64, name="angles")
        cos_in = angles[:, 0]
        sin_turned = angles[:, 1]
        sin_in = const.tile([P, ROUNDS, D], BF16, align_bytes=64, name="sin_in")
        x_in = [inputs.tile([P, GROUP * C], BF16, name="x_g") for g in range(GROUPS)]
        w_raw = {}

        def load_w(third, columns=slice(0, C)):
            if third not in w_raw:
                w_raw[third] = const.tile([P, PACK, C], BF16, name="w_raw%d" % third)
            nc.sync.dma_start(
                out=w_raw[third][:, :, columns], in_=w_view[:, :, third * C + columns.start : third * C + columns.stop]
            )

        def load_x(g, columns=slice(0, GROUP * C)):
            nc.sync.dma_start(out=x_in[g][:, columns], in_=x_view[:, g, columns])

        def load_tables(rounds):
            nc.sync.dma_start(out=cos_in[:, rounds], in_=cos_view[:, rounds])
            nc.sync.dma_start(out=sin_in[:, rounds], in_=sin_view[:, rounds])

        HALF_W = C // 2
        HALF_X = GROUP * C // 2
        load_w(0, slice(0, HALF_W))
        load_x(0, slice(0, HALF_X))
        load_w(0, slice(HALF_W, C))
        load_x(0, slice(HALF_X, 2 * HALF_X))
        load_tables(slice(0, GROUP))
        load_w(1)
        load_w(2)
        load_x(1)
        load_tables(slice(GROUP, 3 * GROUP))
        load_x(2)
        load_x(3)
        load_x(4)
        load_tables(slice(3 * GROUP, ROUNDS))
        for g in range(5, GROUPS):
            load_x(g)

        identity = const.tile([P, P], F32, name="identity")
        make_identity(nc, identity[:])
        identity_bf = const.tile([P, P], BF16, name="identity_bf")
        nc.vector.tensor_copy(out=identity_bf[:], in_=identity[:])
        swap = const.tile([P, P], F32, name="swap")
        nc.vector.tensor_copy(out=swap[:, 0:HALF], in_=identity[:, HALF:D])
        nc.vector.tensor_copy(out=swap[:, HALF:D], in_=identity[:, 0:HALF])


        def turn_sin(rounds):
            first, second = sin_turned[:, rounds, 0:HALF], sin_turned[:, rounds, HALF:D]
            if SINA == 3:
                nc.gpsimd.tensor_scalar(out=first, in0=sin_in[:, rounds, HALF:D], scalar1=1.0, scalar2=0.0, op0=MULT, op1=ADD)
            else:
                nc.scalar.copy(out=first, in_=sin_in[:, rounds, HALF:D])
            if SINA >= 2:
                nc.gpsimd.tensor_scalar(out=second, in0=sin_in[:, rounds, 0:HALF], scalar1=-1.0, scalar2=0.0, op0=MULT, op1=ADD)
            elif SINA == 1:
                nc.scalar.mul(second, sin_in[:, rounds, 0:HALF], -1.0)
            else:
                nc.vector.tensor_scalar(out=second, in0=sin_in[:, rounds, 0:HALF], scalar1=-1.0, scalar2=None, op0=MULT)

        grouped = {}
        x_codes = {}
        tables = {}
        w = {}
        w_grouped = {}

        quantised = {}

        def quantise(name, values, width, columns=None):
            if name not in quantised:
                quantised[name] = (
                    const.tile([P, width], U32, name=name + "_codes", align_bytes=64),
                    const.tile([P, width], U8, name=name + "_scales", align_bytes=64),
                )
            codes, scales = quantised[name]
            c = columns or slice(0, width)
            nc.vector.quantize_mx(
                out=codes[:, c].bitcast(FP8X4), scales=scales[:, c], in_=values[:, c.start * PACK : c.stop * PACK]
            )
            return codes, scales

        x_ordered = {}

        def words_of_x(first, i):
            words = x_in[first + i // 2][:].bitcast(F32).rearrange("p (j m u) -> p j u m", j=GROUP, u=2)
            return words[:, 2 * (i % 2) : 2 * (i % 2) + 2]

        def order_x(first, i):
            ordered = xq.tile([P, 2, 2, P], F32, name="ordered", bufs=3)
            nc.scalar.copy(out=ordered[:], in_=words_of_x(first, i))
            x_ordered[first, i] = ordered[:]

        def turn_x(first, groups, i):
            if i == 0:
                grouped[first] = xq.tile(
                    [P, groups * BANK * PACK],
                    BF16,
                    name="grouped",
                    align_bytes=64,
                    tag="grouped%d" % groups,
                    bufs=3 - groups,
                )
            x_words = x_ordered[first, i] if (first, i) in x_ordered else words_of_x(first, i)
            turned = psum["turned"].tile([P, 2, 2, P], F32, name="turned", tag="turned")
            for j in range(2):
                for u in range(2):
                    nc.tensor.transpose(turned[:, j, u, :], x_words[:, j, u, :], identity[:])
            words = grouped[first][:].bitcast(F32).rearrange("p (j r u) -> p j r u", r=P, u=2)
            nc.scalar.copy(out=words[:, 2 * i : 2 * i + 2], in_=turned[:].rearrange("p j u r -> p j r u"))

        def quantise_x(first, groups, columns=None):
            codes, scales = quantise("x%d" % first, grouped[first], groups * BANK, columns)
            for i in range(groups):
                columns = slice(i * BANK, (i + 1) * BANK)
                x_codes[first + i] = (codes[:, columns], scales[:, columns])

        def turn_tables(g):
            turned = psum["turned"].tile([P, 2, BANK], BF16, name="turned_tables", tag="turned")
            for t, table in enumerate((cos_in, sin_turned)):
                for j in range(GROUP):
                    nc.tensor.transpose(turned[:, t, part(j)], table[:, g * GROUP + j, :], identity_bf[:])
            tables[g] = xq.tile([P, 2, BANK], BF16, name="tables")
            nc.scalar.copy(out=tables[g][:], in_=turned[:])

        def group_w(third, copy, columns=slice(0, C)):
            if third not in w_grouped:
                w_grouped[third] = const.tile([P, BANK * PACK], BF16, align_bytes=64, name="w_grouped%d" % third)
            copy(
                out=w_grouped[third][:, columns.start * PACK : columns.stop * PACK].rearrange("p (c i t) -> p c t i", i=4, t=PACK),
                in_=w_raw[third][:, :, columns].rearrange("p t (c i) -> p c t i", i=4),
            )

        def quantise_w(third, name, columns=None):
            w[name] = quantise("w" + name, w_grouped[third], BANK, columns)

        def part(i):
            return slice(i * P, (i + 1) * P)

        def rounds_of(n):
            return slice(n // HEADS * GROUP, (n // HEADS + 1) * GROUP)

        def multiply(out, stationary, columns, moving, moving_columns):
            nc.tensor.matmul_mx(
                out=out,
                lhsT=stationary[0][:, columns].bitcast(FP8X4),
                lhsT_scale=stationary[1][:, columns],
                rhs=moving[0][:, moving_columns].bitcast(FP8X4),
                rhs_scale=moving[1][:, moving_columns],
                start=True,
                stop=True,
            )

        def pair_of(n):
            rounds = slice(n % PAIR * PAIR, n % PAIR * PAIR + PAIR)
            heads = slice(n // PAIR % PAIR * PAIR, n // PAIR % PAIR * PAIR + PAIR)
            return rounds, heads

        def matmul_pair(n, name, pool=None):
            rounds, heads = pair_of(n)
            if pool:
                acc = psum[pool].tile([P, PAIR, PAIR, D], F32, name=name + "_extra", tag=pool)
            else:
                acc = psum[name + "_acc"].tile([P, PAIR, PAIR, D], F32, name=name + "_acc")
            for i in range(PAIR):
                multiply(
                    acc[:, i].rearrange("p h d -> p (h d)"),
                    x_codes[n // HEADS],
                    part(rounds.start + i),
                    w[name],
                    slice(heads.start * D, heads.stop * D),
                )
            return acc

        def store(view, n, heads, result, rounds=slice(0, GROUP)):
            first = n // HEADS * GROUP
            nc.sync.dma_start(out=view[:, heads, first + rounds.start : first + rounds.stop], in_=result)

        v_out = {}

        def make_v(n, pool=None):
            rounds, heads = pair_of(n)
            acc = matmul_pair(n, "v", pool)
            if n % PAIR == 0:
                v_out[n // PAIR] = work.tile([P, PAIR, GROUP, D], F32, name="v_out", bufs=4)
            nc.scalar.copy(
                out=v_out[n // PAIR][:, :, rounds].rearrange("p h j d -> p j h d"), in_=acc[:]
            )

        q_acc = {}
        q_main = {}
        q_cross = {}

        def sine_on_vector(n):
            return n % 4 != 1 or n >= UNITS - LASTG

        def multiply_q(n):
            if n % PAIR == 0:
                q_main[n // PAIR] = work.tile([P, PAIR, GROUP, D], F32, name="q_main", bufs=6)
                q_cross[n // PAIR] = work.tile([P, PAIR, GROUP, D], F32, name="q_cross", bufs=3)
            rounds, heads = pair_of(n)
            first = n // HEADS * GROUP + rounds.start
            nc.vector.tensor_tensor(
                out=q_main[n // PAIR][:, :, rounds].rearrange("p h j d -> p j h d"),
                in0=q_acc[n][:],
                in1=cos_in[:, first : first + PAIR, :].unsqueeze(2).to_broadcast([P, PAIR, PAIR, D]),
                op=MULT,
            )
            if sine_on_vector(n):
                cross_q(n, q_acc[n], nc.vector)

        def cross_q(n, source, engine):
            rounds, heads = pair_of(n)
            first = n // HEADS * GROUP + rounds.start
            engine.tensor_tensor(
                out=q_cross[n // PAIR][:, :, rounds].rearrange("p h j d -> p j h d"),
                in0=source[:],
                in1=sin_turned[:, first : first + PAIR, :].unsqueeze(2).to_broadcast([P, PAIR, PAIR, D]),
                op=MULT,
            )

        def cross_q_on_gpsimd(n):
            q_raw = work.tile([P, PAIR, PAIR, D], F32, name="q_raw", bufs=4)
            nc.scalar.copy(out=q_raw[:], in_=q_acc[n][:])
            cross_q(n, q_raw, nc.gpsimd)

        def add_crossed(main, crossed, adder):
            main = main.rearrange("p n (f d) -> p n f d", f=2)
            crossed = crossed.rearrange("p n (f d) -> p n f d", f=2)[:, :, ::-1, :]
            adder.tensor_tensor(out=main, in0=main, in1=crossed, op=ADD)

        def add_q(pair, adder):
            add_crossed(
                q_main[pair][:].rearrange("p h j d -> p (h j) d"), q_cross[pair][:].rearrange("p h j d -> p (h j) d"), adder
            )

        k_acc = {}
        k_parts = {}

        def is_turned(n):
            return n % HEADS < TURNED_HEADS or (TAILT and n >= UNITS - HEADS)

        def matmul_k(n):
            if is_turned(n):
                k_acc[n] = psum["k_acc"].tile([P, BANK], F32, name="k_acc")
                multiply(k_acc[n][:], w["k"], part(n % HEADS), x_codes[n // HEADS], slice(0, BANK))
            else:
                k_acc[n] = psum["k_acc"].tile([P, GROUP, D], F32, name="k_acc")
                for j in range(GROUP):
                    multiply(k_acc[n][:, j, :], x_codes[n // HEADS], part(j), w["k"], part(n % HEADS))

        def multiply_k(n):
            acc = k_acc[n]
            if is_turned(n):
                products = work.tile([P, 2, BANK], F32, name="products", bufs=PB)
                nc.vector.tensor_tensor(
                    out=products[:],
                    in0=acc[:].unsqueeze(1).to_broadcast([P, 2, BANK]),
                    in1=tables[n // HEADS][:],
                    op=MULT,
                )
                k_parts[n] = products
            else:
                k_parts[n] = work.tile([P, 2, GROUP, D], F32, name="k_parts", bufs=3)
                nc.vector.tensor_tensor(
                    out=k_parts[n][:],
                    in0=acc[:].unsqueeze(1).to_broadcast([P, 2, GROUP, D]),
                    in1=angles[:, :, rounds_of(n), :],
                    op=MULT,
                )

        def finish_k(n, adder):
            if is_turned(n):
                products = k_parts[n]
                k_sum = psum["turned"].tile([P, GROUP, D], F32, name="k_sum", tag="turned")
                for j in range(GROUP):
                    nc.tensor.matmul(
                        out=k_sum[:, j, :], lhsT=products[:, 0, part(j)], rhs=identity[:], is_transpose=True, start=True, stop=False
                    )
                    nc.tensor.matmul(
                        out=k_sum[:, j, :], lhsT=products[:, 1, part(j)], rhs=swap[:], is_transpose=True, start=False, stop=True
                    )
                k_main = work.tile([P, 1, GROUP, D], F32, name="k_turned", bufs=5)
                nc.scalar.copy(out=k_main[:, 0], in_=k_sum[:])
            else:
                add_crossed(k_parts[n][:, 0], k_parts[n][:, 1], adder)
                return k_parts[n][:, 0:1]
            return k_main[:]

        helpers = {}
        after = {}

        def at(step, task, *args):
            helpers.setdefault(step, []).append((task, args))

        def plan_x(first, groups, steps, quantise_step):
            for i, step in enumerate(steps):
                if step >= 4:
                    at(step - 2, order_x, first, i)
                at(step, turn_x, first, groups, i)
            after.setdefault(quantise_step, []).append((quantise_x, (first, groups)))

        at(GK, group_w, 1, nc.scalar.copy)
        at(QK, quantise_w, 1, "k")
        at(GV, group_w, 2, nc.scalar.copy)
        at(QV, quantise_w, 2, "v")
        for step, rounds in SINS:
            at(step, turn_sin, slice(*rounds))
        for plan in XPLAN:
            plan_x(*plan)
        at(0, turn_tables, 0)
        at(5, turn_tables, 1)
        at(9, turn_tables, 2)
        at(13, turn_tables, 3)
        at(17, turn_tables, 4)
        at(21, turn_tables, 5)
        at(25, turn_tables, 6)
        at(29, turn_tables, 7)

        for i in range(2):
            half = slice(i * BANK // 2, (i + 1) * BANK // 2)
            turn_x(0, 1, i)
            group_w(0, nc.vector.tensor_copy, half)
            quantise_w(0, "q", half)
            quantise_x(0, 1, half)
        turn_sin(slice(0, GROUP))

        pending = {}
        steps = []
        for n in range(UNITS + K_LAG):
            steps.append((n - K_LAG if n >= K_LAG else None, n if n < UNITS else None, n - V_LAG if V_LAG <= n < UNITS + V_LAG else None))
        if TAILSEQ:
            del_ = steps.index((UNITS - 1 - K_LAG, UNITS - 1, UNITS - 1 - V_LAG))
            steps = steps[: del_ - TAILCUT] + list(TAILSEQ)
        steps += [(None, None, None)] * 4
        last_ks = []
        waiting_ks = []
        waiting_turns = []
        q_done = None
        next_v = 0
        for n, (k_, q, v_) in enumerate(steps):
            ks = [k_] if k_ is not None else []
            vs = []
            if n >= V_LAG and next_v < UNITS:
                vs = list(range(next_v, min(UNITS, next_v + 1 + (n in VX))))
                next_v += len(vs)
            for k in ks:
                matmul_k(k)
            if q is not None:
                q_acc[q] = matmul_pair(q, "q")
            for v in vs[:1]:
                make_v(v, VPOOL if VP2 and n >= FS and n % 2 == VP2 - 1 else None)
            for k in ks:
                multiply_k(k)
            if q is not None:
                multiply_q(q)
            for task, args in helpers.get(n, ()):
                if task in (turn_x, turn_tables) and n >= FS:
                    waiting_turns.append((task, args))
                else:
                    task(*args)
            flush = n < FS or n % 2 == FP or n >= FE
            if flush:
                for task, args in waiting_turns:
                    task(*args)
                waiting_turns = []
            for task, args in after.get(n, ()):
                task(*args)
            rest = []
            for k in waiting_ks + last_ks:
                if is_turned(k) and not flush:
                    rest.append(k)
                    continue
                k_main = finish_k(k, nc.gpsimd)
                pending.setdefault(n + (0 if is_turned(k) else 2), []).append((k_view, k, slice(k % HEADS, k % HEADS + 1), k_main, slice(0, GROUP)))
            waiting_ks = rest
            last_ks = ks
            for v in vs[1:]:
                make_v(v, VPOOL)
            if q is not None and not sine_on_vector(q):
                cross_q_on_gpsimd(q)
            for v in vs:
                if v % PAIR == PAIR - 1:
                    store(v_view, v, pair_of(v)[1], v_out[v // PAIR][:])
            unit = q_done
            if unit is not None and TAILG and unit >= UNITS - 2:
                pair = unit // PAIR
                rounds, heads = pair_of(unit)
                last = unit == UNITS - 1
                for h in range(PAIR):
                    add_crossed(q_main[pair][:, h, rounds], q_cross[pair][:, h, rounds], nc.vector if last else nc.gpsimd)
                if TAILS:
                    pending.setdefault(n + (0 if last else 1), []).append((q_view, unit, heads, q_main[pair][:, :, rounds], rounds))
                elif last:
                    pending.setdefault(n, []).append((q_view, unit, heads, q_main[pair][:], slice(0, GROUP)))
            elif unit is not None and unit % PAIR == PAIR - 1:
                pair = unit // PAIR
                add_q(pair, nc.vector if unit == UNITS - 1 else nc.gpsimd)
                pending.setdefault(n + (0 if unit == UNITS - 1 else SPQ), []).append((q_view, unit, pair_of(unit)[1], q_main[pair][:], slice(0, GROUP)))
            q_done = q
            for view, unit, heads, result, rounds in pending.get(n, ()):
                store(view, unit, heads, result, rounds)
